import numpy as np
import ml_dtypes


def mxq(x, axis, fmt="e4m3"):
    dtype, down = {"e4m3": (ml_dtypes.float8_e4m3fn, 7), "e5m2": (ml_dtypes.float8_e5m2, 14)}[fmt]
    v = np.moveaxis(np.asarray(x, np.float32).astype(ml_dtypes.bfloat16).astype(np.float64), axis, -1)
    blocks = v.reshape(v.shape[:-1] + (-1, 32))
    amax = np.abs(blocks).max(-1, keepdims=True)
    byte = np.maximum(np.where(amax > 0, np.frexp(amax)[1] - 1 + 127, 0) - down, 1)
    scale = np.exp2(byte - 127.0)
    codes = (blocks / scale).astype(np.float32).astype(dtype).astype(np.float64)
    return np.moveaxis((codes * scale).reshape(v.shape), -1, axis)


WIDE = False


def mx_kscale(k):
    if not WIDE:
        return np.ones(k)
    levels = np.array([10, -10, 5, -5, 0])
    a = np.random.permutation(np.resize(levels, k // 512 * 4)).reshape(k // 512, 4)
    idx = np.arange(k)
    return np.exp2(a[idx // 512, idx % 128 // 32])


BF16 = ml_dtypes.bfloat16


def bf(x):
    return np.asarray(x, np.float32).astype(BF16)


def f64(x):
    return np.asarray(x).astype(np.float64)


B, H, N, D = 1, 16, 1024, 128
NEG_INF = -1.0e12


def setup_inputs():
    s = mx_kscale(N)
    Q = np.random.standard_normal((B, H, N, D)) * 1.5
    K = np.random.standard_normal((B, H, N, D))
    V = np.random.standard_normal((B, H, N, D)) * 2.0 * (s.max() / s)[:, None]
    Q[..., 0] = 8.0
    K[..., 0] = (np.log(s) + 0.5 * K[..., 0]) * np.sqrt(D) / 8.0
    return {"Q": bf(Q), "K": bf(K), "V": bf(V), "mask": np.random.random_sample((N, N)) < 0.5}


def reference(Q, K, V, mask):
    score = f64(Q) @ f64(K).transpose(0, 1, 3, 2) / np.sqrt(D)
    score = np.where(mask, NEG_INF, score)
    e = np.exp(score - score.max(-1, keepdims=True))
    return (mxq(e, 3, "e4m3") @ mxq(f64(V), 2, "e4m3")) / e.sum(-1, keepdims=True)

@@ -1,0 +1,212 @@
+import math
+from contextlib import ExitStack
+
+import concourse.mybir as mybir
+from concourse.masks import make_identity
+
+FP8X4 = mybir.dt.float8_e4m3fn_x4
+BF16 = mybir.dt.bfloat16
+F32 = mybir.dt.float32
+I32 = mybir.dt.int32
+U32 = mybir.dt.uint32
+U8 = mybir.dt.uint8
+ALU = mybir.AluOpType
+ACTF = mybir.ActivationFunctionType
+
+P = 128
+H = 16
+N = 1024
+D = 128
+NJ = N // P
+PACK = 4
+G = N // (P * PACK)
+GT = G * PACK
+UB = 4
+SCALE = 1.0 / math.sqrt(D)
+MASK_RAW = -1.0e12 * math.sqrt(D)
+FLOPS = 4 * H * N * N * D
+
+V_TAKES = (1, 3, 5, 6, 7)
+
+
+def tile_scaleddotproductattention_kernel(tc, Q, K, V, mask, out):
+    nc = tc.nc
+    with ExitStack() as ctx:
+        const = ctx.enter_context(tc.tile_pool(name="const", bufs=1))
+        mstage = ctx.enter_context(tc.tile_pool(name="mstage", bufs=2))
+        raw = ctx.enter_context(tc.tile_pool(name="raw", bufs=3))
+        heads = ctx.enter_context(tc.tile_pool(name="heads", bufs=2))
+        work = ctx.enter_context(tc.tile_pool(name="work", bufs=3))
+        small = ctx.enter_context(tc.tile_pool(name="small", bufs=6))
+        batch = ctx.enter_context(tc.tile_pool(name="batch", bufs=2))
+        ps_s = ctx.enter_context(tc.psum_pool(name="ps_s", bufs=4))
+        ps_e = ctx.enter_context(tc.psum_pool(name="ps_e", bufs=2))
+        ps_o = ctx.enter_context(tc.psum_pool(name="ps_o", bufs=1))
+        ps_t = ctx.enter_context(tc.psum_pool(name="ps_t", bufs=1))
+
+        ident_bf = const.tile([P, P], BF16)
+        make_identity(nc, ident_bf[:])
+        ident_f = const.tile([P, P], F32)
+        make_identity(nc, ident_f[:])
+        mask_t = const.tile([P, GT, NJ, P], F32)
+
+        mask_words = mask.bitcast(I32).rearrange("(p j) w -> p j w", j=NJ)
+
+        def load_head(h):
+            k_sb = raw.tile([P, G, PACK, D], BF16, tag="k_sb")
+            nc.sync.dma_start(out=k_sb[:], in_=K[0, h].rearrange("(g p t) d -> p g t d", g=G, t=PACK))
+            q_sb = raw.tile([P, NJ, D], BF16, tag="q_sb")
+            nc.sync.dma_start(out=q_sb[:], in_=Q[0, h].rearrange("(p j) d -> p j d", j=NJ))
+            v_sb = raw.tile([P, G, PACK, D], BF16, tag="v_sb")
+            nc.sync.dma_start(out=v_sb[:], in_=V[0, h].rearrange("(g p t) d -> p g t d", g=G, t=PACK))
+            return k_sb, q_sb, v_sb
+
+        def prep_head(k_sb, q_sb, v_sb):
+            pk = ps_t.tile([P, GT, P], BF16, tag="tr")
+            for g in range(G):
+                for t in range(PACK):
+                    nc.tensor.transpose(out=pk[:, g * PACK + t, :], in_=k_sb[:, g, t, :], identity=ident_bf[:])
+            k_t = heads.tile([P, N], BF16, tag="k_t")
+            nc.scalar.copy(out=k_t[:], in_=pk[:].rearrange("d c p -> d (c p)"))
+            pq = ps_t.tile([P, NJ, P], BF16, tag="tr")
+            for j in range(NJ):
+                nc.tensor.transpose(out=pq[:, j, :], in_=q_sb[:, j, :], identity=ident_bf[:])
+            q_t = heads.tile([P, NJ, P], BF16, tag="q_t")
+            nc.vector.tensor_copy(out=q_t[:], in_=pq[:])
+            v_g = heads.tile([P, G, D, PACK], BF16, tag="v_g", align_bytes=64)
+            nc.gpsimd.tensor_scalar(
+                out=v_g[:],
+                in0=v_sb[:].rearrange("p g t d -> p g d t"),
+                scalar1=1.0,
+                scalar2=0.0,
+                op0=ALU.mult,
+                op1=ALU.add,
+            )
+            v_codes = heads.tile([P, G * D], U32, tag="v_codes", align_bytes=64)
+            v_scales = heads.tile([P, G * D], U8, tag="v_scales", align_bytes=64)
+            nc.vector.quantize_mx(
+                out=v_codes[:].bitcast(FP8X4),
+                scales=v_scales[:],
+                in_=v_g[:].rearrange("p g d t -> p (g d t)"),
+            )
+            return k_t, q_t, v_codes, v_scales
+
+        def prep_mask(j):
+            mi = mstage.tile([P, 2 * N], I32, tag="mi")
+            nc.sync.dma_start(out=mi[:], in_=mask_words[:, j, :])
+            mf = mstage.tile([P, G, PACK, P], F32, tag="mf")
+            nc.vector.tensor_scalar(
+                out=mf[:],
+                in0=mi[:].rearrange("q (g p t w) -> q g t p w", g=G, p=P, t=PACK, w=2)[:, :, :, :, 0],
+                scalar1=MASK_RAW,
+                scalar2=None,
+                op0=ALU.mult,
+            )
+            for g in range(G):
+                pm = ps_t.tile([P, PACK, P], F32, tag="tr")
+                for t in range(PACK):
+                    nc.tensor.transpose(out=pm[:, t, :], in_=mf[:, g, t, :], identity=ident_f[:])
+                nc.scalar.copy(out=mask_t[:, g * PACK : (g + 1) * PACK, j, :], in_=pm[:])
+
+        loaded = load_head(0)
+        for h in range(H):
+            k_t, q_t, v_codes, v_scales = prep_head(*loaded)
+            if h + 1 < H:
+                loaded = load_head(h + 1)
+            out_h = out[0, h].rearrange("(p j) d -> p j d", j=NJ)
+            for b in range(NJ // UB):
+                grouped = batch.tile([P, G, UB * P, PACK], BF16, tag="grouped", align_bytes=64)
+                rowsum = batch.tile([P, UB], F32, tag="rowsum")
+                for u in range(UB):
+                    j = b * UB + u
+                    if h == 0:
+                        prep_mask(j)
+                    banks = []
+                    for g in range(G):
+                        sp = ps_s.tile([P, PACK * P], F32, tag="s")
+                        for t in range(PACK):
+                            nc.tensor.matmul(
+                                out=sp[:, t * P : (t + 1) * P],
+                                lhsT=mask_t[:, g * PACK + t, j, :],
+                                rhs=ident_f[:],
+                                is_transpose=True,
+                                start=(t == 0),
+                                stop=False,
+                            )
+                        nc.tensor.matmul(
+                            out=sp[:],
+                            lhsT=q_t[:, j, :],
+                            rhs=k_t[:, g * PACK * P : (g + 1) * PACK * P],
+                            start=False,
+                            stop=True,
+                        )
+                        banks.append(sp)
+                    neg_s = work.tile([P, G, PACK * P], F32, tag="neg_s")
+                    neg_m0 = small.tile([P, 1], F32, tag="neg_m0")
+                    neg_m = small.tile([P, 1], F32, tag="neg_m")
+                    nc.vector.tensor_scalar(
+                        out=neg_s[:, 0, :],
+                        in0=banks[0][:],
+                        scalar1=-SCALE,
+                        scalar2=None,
+                        op0=ALU.mult,
+                        op1=ALU.min,
+                        accum_out=neg_m0[:],
+                    )
+                    nc.vector.tensor_scalar(
+                        out=neg_s[:, 1, :],
+                        in0=banks[1][:],
+                        scalar1=-SCALE,
+                        scalar2=neg_m0[:, 0:1],
+                        op0=ALU.mult,
+                        op1=ALU.min,
+                        accum_out=neg_m[:],
+                    )
+                    e = work.tile([P, N], BF16, tag="e")
+                    nc.scalar.activation(
+                        out=e[:],
+                        in_=neg_s[:].rearrange("q g c -> q (g c)"),
+                        func=ACTF.Exp,
+                        bias=neg_m[:, 0:1],
+                        scale=-1.0,
+                        accum_out=rowsum[:, u : u + 1],
+                    )
+                    et = ps_e.tile([P, GT, P], BF16, tag="et")
+                    for c in range(GT):
+                        nc.tensor.transpose(out=et[:, c, :], in_=e[:, c * P : (c + 1) * P], identity=ident_bf[:])
+                    for g in range(G):
+                        dst = grouped[:, g, u * P : (u + 1) * P, :]
+                        src = et[:, g * PACK : (g + 1) * PACK, :].rearrange("p t q -> p q t")
+                        if g == 1 and j in V_TAKES:
+                            nc.vector.tensor_copy(out=dst, in_=src)
+                        else:
+                            nc.scalar.copy(out=dst, in_=src)
+                codes = batch.tile([P, G, UB * P], U32, tag="codes", align_bytes=64)
+                scales = batch.tile([P, G, UB * P], U8, tag="scales", align_bytes=64)
+                nc.vector.quantize_mx(
+                    out=codes[:].rearrange("p g q -> p (g q)").bitcast(FP8X4),
+                    scales=scales[:].rearrange("p g q -> p (g q)"),
+                    in_=grouped[:].rearrange("p g q t -> p (g q t)"),
+                )
+                o_ps = ps_o.tile([P, UB, D], F32, tag="o")
+                for u in range(UB):
+                    for g in range(G):
+                        nc.tensor.matmul_mx(
+                            out=o_ps[:, u, :],
+                            lhsT=codes[:, g, u * P : (u + 1) * P].bitcast(FP8X4),
+                            lhsT_scale=scales[:, g, u * P : (u + 1) * P],
+                            rhs=v_codes[:, g * D : (g + 1) * D].bitcast(FP8X4),
+                            rhs_scale=v_scales[:, g * D : (g + 1) * D],
+                            start=(g == 0),
+                            stop=(g == G - 1),
+                        )
+                rinv = batch.tile([P, UB], F32, tag="rinv")
+                nc.vector.reciprocal(out=rinv[:], in_=rowsum[:])
+                o_sb = batch.tile([P, UB, D], F32, tag="o_sb")
+                nc.vector.tensor_tensor(
+                    out=o_sb[:],
+                    in0=o_ps[:],
+                    in1=rinv[:].unsqueeze(2).to_broadcast([P, UB, D]),
+                    op=ALU.mult,
+                )
+                nc.sync.dma_start(out=out_h[:, b * UB : (b + 1) * UB, :], in_=o_sb[:])

@@ -22,11 +22,11 @@ PACK = 4
 G = N // (P * PACK)
 GT = G * PACK
 UB = 4
+UNITS = H * NJ
+BATCHES = UNITS // UB
 SCALE = 1.0 / math.sqrt(D)
 MASK_RAW = -1.0e12 * math.sqrt(D)
 FLOPS = 4 * H * N * N * D
-
-V_TAKES = (1, 3, 5, 6, 7)
 
 
 def tile_scaleddotproductattention_kernel(tc, Q, K, V, mask, out):
@@ -35,178 +35,304 @@ def tile_scaleddotproductattention_kernel(tc, Q, K, V, mask, out):
         const = ctx.enter_context(tc.tile_pool(name="const", bufs=1))
         mstage = ctx.enter_context(tc.tile_pool(name="mstage", bufs=2))
         raw = ctx.enter_context(tc.tile_pool(name="raw", bufs=3))
-        heads = ctx.enter_context(tc.tile_pool(name="heads", bufs=2))
+        heads = ctx.enter_context(tc.tile_pool(name="heads", bufs=3))
         work = ctx.enter_context(tc.tile_pool(name="work", bufs=3))
-        small = ctx.enter_context(tc.tile_pool(name="small", bufs=6))
-        batch = ctx.enter_context(tc.tile_pool(name="batch", bufs=2))
+        small = ctx.enter_context(tc.tile_pool(name="small", bufs=4))
+        batch = ctx.enter_context(tc.tile_pool(name="batch", bufs=3))
         ps_s = ctx.enter_context(tc.psum_pool(name="ps_s", bufs=4))
         ps_e = ctx.enter_context(tc.psum_pool(name="ps_e", bufs=2))
         ps_o = ctx.enter_context(tc.psum_pool(name="ps_o", bufs=1))
         ps_t = ctx.enter_context(tc.psum_pool(name="ps_t", bufs=1))
+        ctx.enter_context(tc.manual_schedule())
 
         ident_bf = const.tile([P, P], BF16)
         make_identity(nc, ident_bf[:])
         ident_f = const.tile([P, P], F32)
         make_identity(nc, ident_f[:])
         mask_t = const.tile([P, GT, NJ, P], F32)
-
         mask_words = mask.bitcast(I32).rearrange("(p j) w -> p j w", j=NJ)
+
+        st = {}
 
         def load_head(h):
             k_sb = raw.tile([P, G, PACK, D], BF16, tag="k_sb")
             nc.sync.dma_start(out=k_sb[:], in_=K[0, h].rearrange("(g p t) d -> p g t d", g=G, t=PACK))
             q_sb = raw.tile([P, NJ, D], BF16, tag="q_sb")
             nc.sync.dma_start(out=q_sb[:], in_=Q[0, h].rearrange("(p j) d -> p j d", j=NJ))
+            st["k_sb", h] = k_sb
+            st["q_sb", h] = q_sb
+
+        def load_v(h):
             v_sb = raw.tile([P, G, PACK, D], BF16, tag="v_sb")
             nc.sync.dma_start(out=v_sb[:], in_=V[0, h].rearrange("(g p t) d -> p g t d", g=G, t=PACK))
-            return k_sb, q_sb, v_sb
+            st["v_sb", h] = v_sb
 
-        def prep_head(k_sb, q_sb, v_sb):
+        def k_transposes(h):
             pk = ps_t.tile([P, GT, P], BF16, tag="tr")
+            k_sb = st["k_sb", h]
             for g in range(G):
                 for t in range(PACK):
                     nc.tensor.transpose(out=pk[:, g * PACK + t, :], in_=k_sb[:, g, t, :], identity=ident_bf[:])
+            st["pk", h] = pk
+
+        def k_copy(h):
             k_t = heads.tile([P, N], BF16, tag="k_t")
-            nc.scalar.copy(out=k_t[:], in_=pk[:].rearrange("d c p -> d (c p)"))
+            nc.scalar.copy(out=k_t[:], in_=st["pk", h][:].rearrange("d c p -> d (c p)"))
+            st["k_t", h] = k_t
+
+        def q_transposes(h):
             pq = ps_t.tile([P, NJ, P], BF16, tag="tr")
+            q_sb = st["q_sb", h]
             for j in range(NJ):
                 nc.tensor.transpose(out=pq[:, j, :], in_=q_sb[:, j, :], identity=ident_bf[:])
+            st["pq", h] = pq
+
+        def q_copy(h):
             q_t = heads.tile([P, NJ, P], BF16, tag="q_t")
-            nc.vector.tensor_copy(out=q_t[:], in_=pq[:])
+            nc.vector.tensor_copy(out=q_t[:], in_=st["pq", h][:])
+            st["q_t", h] = q_t
+
+        def v_group(h):
             v_g = heads.tile([P, G, D, PACK], BF16, tag="v_g", align_bytes=64)
             nc.gpsimd.tensor_scalar(
                 out=v_g[:],
-                in0=v_sb[:].rearrange("p g t d -> p g d t"),
+                in0=st["v_sb", h][:].rearrange("p g t d -> p g d t"),
                 scalar1=1.0,
                 scalar2=0.0,
                 op0=ALU.mult,
                 op1=ALU.add,
             )
+            st["v_g", h] = v_g
+
+        def v_quantise(h):
             v_codes = heads.tile([P, G * D], U32, tag="v_codes", align_bytes=64)
             v_scales = heads.tile([P, G * D], U8, tag="v_scales", align_bytes=64)
             nc.vector.quantize_mx(
                 out=v_codes[:].bitcast(FP8X4),
                 scales=v_scales[:],
-                in_=v_g[:].rearrange("p g d t -> p (g d t)"),
+                in_=st["v_g", h][:].rearrange("p g d t -> p (g d t)"),
             )
-            return k_t, q_t, v_codes, v_scales
+            st["v_codes", h] = v_codes
+            st["v_scales", h] = v_scales
 
-        def prep_mask(j):
-            mi = mstage.tile([P, 2 * N], I32, tag="mi")
+        def mask_load(j):
+            mi = mstage.tile([P, 2 * N], I32, tag="mi", bufs=4)
             nc.sync.dma_start(out=mi[:], in_=mask_words[:, j, :])
+            st["mi", j] = mi
+
+        def mask_convert(j):
             mf = mstage.tile([P, G, PACK, P], F32, tag="mf")
             nc.vector.tensor_scalar(
                 out=mf[:],
-                in0=mi[:].rearrange("q (g p t w) -> q g t p w", g=G, p=P, t=PACK, w=2)[:, :, :, :, 0],
+                in0=st["mi", j][:].rearrange("q (g p t w) -> q g t p w", g=G, p=P, t=PACK, w=2)[:, :, :, :, 0],
                 scalar1=MASK_RAW,
                 scalar2=None,
                 op0=ALU.mult,
             )
-            for g in range(G):
-                pm = ps_t.tile([P, PACK, P], F32, tag="tr")
-                for t in range(PACK):
-                    nc.tensor.transpose(out=pm[:, t, :], in_=mf[:, g, t, :], identity=ident_f[:])
-                nc.scalar.copy(out=mask_t[:, g * PACK : (g + 1) * PACK, j, :], in_=pm[:])
+            st["mf", j] = mf
 
-        loaded = load_head(0)
-        for h in range(H):
-            k_t, q_t, v_codes, v_scales = prep_head(*loaded)
-            if h + 1 < H:
-                loaded = load_head(h + 1)
+        def mask_transposes(j, g):
+            pm = ps_t.tile([P, PACK, P], F32, tag="tr")
+            for t in range(PACK):
+                nc.tensor.transpose(out=pm[:, t, :], in_=st["mf", j][:, g, t, :], identity=ident_f[:])
+            st["pm", j, g] = pm
+
+        def mask_copy(j, g):
+            nc.scalar.copy(out=mask_t[:, g * PACK : (g + 1) * PACK, j, :], in_=st["pm", j, g][:])
+
+        def scores(i, g):
+            h, j = divmod(i, NJ)
+            sp = ps_s.tile([P, PACK * P], F32, tag="s")
+            for t in range(PACK):
+                nc.tensor.matmul(
+                    out=sp[:, t * P : (t + 1) * P],
+                    lhsT=mask_t[:, g * PACK + t, j, :],
+                    rhs=ident_f[:],
+                    is_transpose=True,
+                    start=(t == 0),
+                    stop=False,
+                )
+            nc.tensor.matmul(
+                out=sp[:],
+                lhsT=st["q_t", h][:, j, :],
+                rhs=st["k_t", h][:, g * PACK * P : (g + 1) * PACK * P],
+                start=False,
+                stop=True,
+            )
+            st["sp", i, g] = sp
+
+        def row_max(i):
+            neg_s = work.tile([P, G, PACK * P], F32, tag="neg_s")
+            neg_m0 = small.tile([P, 1], F32, tag="neg_m0")
+            neg_m = small.tile([P, 1], F32, tag="neg_m")
+            nc.vector.tensor_scalar(
+                out=neg_s[:, 0, :],
+                in0=st["sp", i, 0][:],
+                scalar1=-SCALE,
+                scalar2=None,
+                op0=ALU.mult,
+                op1=ALU.min,
+                accum_out=neg_m0[:],
+            )
+            nc.vector.tensor_scalar(
+                out=neg_s[:, 1, :],
+                in0=st["sp", i, 1][:],
+                scalar1=-SCALE,
+                scalar2=neg_m0[:, 0:1],
+                op0=ALU.mult,
+                op1=ALU.min,
+                accum_out=neg_m[:],
+            )
+            st["neg_s", i] = neg_s
+            st["neg_m", i] = neg_m
+
+        def exponent(i):
+            b, u = divmod(i, UB)
+            if u == 0:
+                st["rowsum", b] = batch.tile([P, UB], F32, tag="rowsum", name="rowsum", bufs=4)
+            e = work.tile([P, N], BF16, tag="e")
+            nc.scalar.activation(
+                out=e[:],
+                in_=st["neg_s", i][:].rearrange("q g c -> q (g c)"),
+                func=ACTF.Exp,
+                bias=st["neg_m", i][:, 0:1],
+                scale=-1.0,
+                accum_out=st["rowsum", b][:, u : u + 1],
+            )
+            st["e", i] = e
+
+        def e_transposes(i, lo, hi):
+            if lo == 0:
+                st["et", i] = ps_e.tile([P, GT, P], BF16, tag="et", name="et")
+            for c in range(lo, hi):
+                nc.tensor.transpose(
+                    out=st["et", i][:, c, :], in_=st["e", i][:, c * P : (c + 1) * P], identity=ident_bf[:]
+                )
+
+        def e_copy(i):
+            ec = work.tile([P, GT, P], BF16, tag="ec")
+            nc.scalar.copy(out=ec[:], in_=st["et", i][:])
+            st["ec", i] = ec
+
+        def e_group(i):
+            b, u = divmod(i, UB)
+            if u == 0:
+                st["grouped", b] = batch.tile(
+                    [P, G, UB * P, PACK], BF16, tag="grouped", name="grouped", align_bytes=64
+                )
+            nc.gpsimd.tensor_scalar(
+                out=st["grouped", b][:, :, u * P : (u + 1) * P, :],
+                in0=st["ec", i][:].rearrange("p (g t) q -> p g q t", g=G),
+                scalar1=1.0,
+                scalar2=0.0,
+                op0=ALU.mult,
+                op1=ALU.add,
+            )
+
+        def e_quantise(b):
+            codes = batch.tile([P, G, UB * P], U32, tag="codes", align_bytes=64)
+            scales = batch.tile([P, G, UB * P], U8, tag="scales", align_bytes=64)
+            nc.vector.quantize_mx(
+                out=codes[:].rearrange("p g q -> p (g q)").bitcast(FP8X4),
+                scales=scales[:].rearrange("p g q -> p (g q)"),
+                in_=st["grouped", b][:].rearrange("p g q t -> p (g q t)"),
+            )
+            st["codes", b] = codes
+            st["scales", b] = scales
+
+        def pv(b):
+            h = b // (NJ // UB)
+            o_ps = ps_o.tile([P, UB, D], F32, tag="o")
+            for u in range(UB):
+                for g in range(G):
+                    nc.tensor.matmul_mx(
+                        out=o_ps[:, u, :],
+                        lhsT=st["codes", b][:, g, u * P : (u + 1) * P].bitcast(FP8X4),
+                        lhsT_scale=st["scales", b][:, g, u * P : (u + 1) * P],
+                        rhs=st["v_codes", h][:, g * D : (g + 1) * D].bitcast(FP8X4),
+                        rhs_scale=st["v_scales", h][:, g * D : (g + 1) * D],
+                        start=(g == 0),
+                        stop=(g == G - 1),
+                    )
+            st["o_ps", b] = o_ps
+
+        def normalise(b):
+            h, half = divmod(b, NJ // UB)
+            rinv = batch.tile([P, UB], F32, tag="rinv")
+            nc.vector.reciprocal(out=rinv[:], in_=st["rowsum", b][:])
+            o_sb = batch.tile([P, UB, D], F32, tag="o_sb")
+            nc.vector.tensor_tensor(
+                out=o_sb[:],
+                in0=st["o_ps", b][:],
+                in1=rinv[:].unsqueeze(2).to_broadcast([P, UB, D]),
+                op=ALU.mult,
+            )
             out_h = out[0, h].rearrange("(p j) d -> p j d", j=NJ)
-            for b in range(NJ // UB):
-                grouped = batch.tile([P, G, UB * P, PACK], BF16, tag="grouped", align_bytes=64)
-                rowsum = batch.tile([P, UB], F32, tag="rowsum")
-                for u in range(UB):
-                    j = b * UB + u
-                    if h == 0:
-                        prep_mask(j)
-                    banks = []
-                    for g in range(G):
-                        sp = ps_s.tile([P, PACK * P], F32, tag="s")
-                        for t in range(PACK):
-                            nc.tensor.matmul(
-                                out=sp[:, t * P : (t + 1) * P],
-                                lhsT=mask_t[:, g * PACK + t, j, :],
-                                rhs=ident_f[:],
-                                is_transpose=True,
-                                start=(t == 0),
-                                stop=False,
-                            )
-                        nc.tensor.matmul(
-                            out=sp[:],
-                            lhsT=q_t[:, j, :],
-                            rhs=k_t[:, g * PACK * P : (g + 1) * PACK * P],
-                            start=False,
-                            stop=True,
-                        )
-                        banks.append(sp)
-                    neg_s = work.tile([P, G, PACK * P], F32, tag="neg_s")
-                    neg_m0 = small.tile([P, 1], F32, tag="neg_m0")
-                    neg_m = small.tile([P, 1], F32, tag="neg_m")
-                    nc.vector.tensor_scalar(
-                        out=neg_s[:, 0, :],
-                        in0=banks[0][:],
-                        scalar1=-SCALE,
-                        scalar2=None,
-                        op0=ALU.mult,
-                        op1=ALU.min,
-                        accum_out=neg_m0[:],
-                    )
-                    nc.vector.tensor_scalar(
-                        out=neg_s[:, 1, :],
-                        in0=banks[1][:],
-                        scalar1=-SCALE,
-                        scalar2=neg_m0[:, 0:1],
-                        op0=ALU.mult,
-                        op1=ALU.min,
-                        accum_out=neg_m[:],
-                    )
-                    e = work.tile([P, N], BF16, tag="e")
-                    nc.scalar.activation(
-                        out=e[:],
-                        in_=neg_s[:].rearrange("q g c -> q (g c)"),
-                        func=ACTF.Exp,
-                        bias=neg_m[:, 0:1],
-                        scale=-1.0,
-                        accum_out=rowsum[:, u : u + 1],
-                    )
-                    et = ps_e.tile([P, GT, P], BF16, tag="et")
-                    for c in range(GT):
-                        nc.tensor.transpose(out=et[:, c, :], in_=e[:, c * P : (c + 1) * P], identity=ident_bf[:])
-                    for g in range(G):
-                        dst = grouped[:, g, u * P : (u + 1) * P, :]
-                        src = et[:, g * PACK : (g + 1) * PACK, :].rearrange("p t q -> p q t")
-                        if g == 1 and j in V_TAKES:
-                            nc.vector.tensor_copy(out=dst, in_=src)
-                        else:
-                            nc.scalar.copy(out=dst, in_=src)
-                codes = batch.tile([P, G, UB * P], U32, tag="codes", align_bytes=64)
-                scales = batch.tile([P, G, UB * P], U8, tag="scales", align_bytes=64)
-                nc.vector.quantize_mx(
-                    out=codes[:].rearrange("p g q -> p (g q)").bitcast(FP8X4),
-                    scales=scales[:].rearrange("p g q -> p (g q)"),
-                    in_=grouped[:].rearrange("p g q t -> p (g q t)"),
-                )
-                o_ps = ps_o.tile([P, UB, D], F32, tag="o")
-                for u in range(UB):
-                    for g in range(G):
-                        nc.tensor.matmul_mx(
-                            out=o_ps[:, u, :],
-                            lhsT=codes[:, g, u * P : (u + 1) * P].bitcast(FP8X4),
-                            lhsT_scale=scales[:, g, u * P : (u + 1) * P],
-                            rhs=v_codes[:, g * D : (g + 1) * D].bitcast(FP8X4),
-                            rhs_scale=v_scales[:, g * D : (g + 1) * D],
-                            start=(g == 0),
-                            stop=(g == G - 1),
-                        )
-                rinv = batch.tile([P, UB], F32, tag="rinv")
-                nc.vector.reciprocal(out=rinv[:], in_=rowsum[:])
-                o_sb = batch.tile([P, UB, D], F32, tag="o_sb")
-                nc.vector.tensor_tensor(
-                    out=o_sb[:],
-                    in0=o_ps[:],
-                    in1=rinv[:].unsqueeze(2).to_broadcast([P, UB, D]),
-                    op=ALU.mult,
-                )
-                nc.sync.dma_start(out=out_h[:, b * UB : (b + 1) * UB, :], in_=o_sb[:])
+            nc.sync.dma_start(out=out_h[:, half * UB : (half + 1) * UB, :], in_=o_sb[:])
+
+        def prep_step(h):
+            return -2 if h == 0 else (NJ - 1 if h == 1 else NJ * h - 2)
+
+        prep_at = dict((prep_step(h), h) for h in range(H))
+
+        load_head(0)
+        mask_load(0)
+        mask_load(1)
+        load_v(0)
+        mask_load(2)
+
+        for k in range(-2, UNITS + 12):
+            if 3 <= k + 5 < NJ:
+                mask_load(k + 5)
+            if k == 3:
+                load_head(1)
+                load_v(1)
+            if k >= 3 and (k - 3) % NJ == 0 and 2 <= (k - 3) // NJ + 2 < H:
+                load_head((k - 3) // NJ + 2)
+                load_v((k - 3) // NJ + 2)
+            hp = prep_at.get(k)
+            hq = prep_at.get(k - 1)
+            if 0 <= k < NJ:
+                mask_copy(k, 1)
+            if hq is not None:
+                q_copy(hq)
+            if 0 <= k + 1 < NJ:
+                mask_transposes(k + 1, 0)
+            if hp is not None:
+                k_transposes(hp)
+            if 0 <= k < UNITS:
+                scores(k, 0)
+            if 0 <= k - 3 < UNITS:
+                e_transposes(k - 3, 0, GT // 2)
+            if 0 <= k - 1 < UNITS:
+                row_max(k - 1)
+            if 0 <= k - 2 < UNITS:
+                exponent(k - 2)
+            if 0 <= k + 1 < NJ:
+                mask_copy(k + 1, 0)
+            if hp is not None:
+                k_copy(hp)
+            if 0 <= k < UNITS:
+                scores(k, 1)
+            if (k - 10) % UB == 0 and 0 <= (k - 10) // UB < BATCHES:
+                pv((k - 10) // UB)
+            if 0 <= k - 3 < UNITS:
+                e_transposes(k - 3, GT // 2, GT)
+            if 0 <= k + 1 < NJ:
+                mask_transposes(k + 1, 1)
+            if hp is not None:
+                q_transposes(hp)
+            if 0 <= k - 4 < UNITS:
+                e_copy(k - 4)
+            if 0 <= k - 5 < UNITS:
+                e_group(k - 5)
+            if hp is not None:
+                v_group(hp)
+            if (k - 9) % UB == 0 and 0 <= (k - 9) // UB < BATCHES:
+                e_quantise((k - 9) // UB)
+            if (k - 11) % UB == 0 and 0 <= (k - 11) // UB < BATCHES:
+                normalise((k - 11) // UB)
+            if hq is not None:
+                v_quantise(hq)
+            if 0 <= k + 2 < NJ:
+                mask_convert(k + 2)

@@ -26,7 +26,10 @@ UNITS = H * NJ
 BATCHES = UNITS // UB
 SCALE = 1.0 / math.sqrt(D)
 MASK_RAW = -1.0e12 * math.sqrt(D)
+MASK_SCALED = 1.0e12
 FLOPS = 4 * H * N * N * D
+V_MASKED = (1, 3, 5, 7)
+T_MASKED = (0, 2, 4, 6)
 
 
 def tile_scaleddotproductattention_kernel(tc, Q, K, V, mask, out):
@@ -49,7 +52,8 @@ def tile_scaleddotproductattention_kernel(tc, Q, K, V, mask, out):
         make_identity(nc, ident_bf[:])
         ident_f = const.tile([P, P], F32)
         make_identity(nc, ident_f[:])
-        mask_t = const.tile([P, GT, NJ, P], F32)
+        mask_t = const.tile([P, GT, NJ - len(V_MASKED), P], F32)
+        mask_a = const.tile([P, len(V_MASKED), G, PACK * P], BF16)
         mask_words = mask.bitcast(I32).rearrange("(p j) w -> p j w", j=NJ)
 
         st = {}
@@ -89,19 +93,12 @@ def tile_scaleddotproductattention_kernel(tc, Q, K, V, mask, out):
 
         def q_copy(h):
             q_t = heads.tile([P, NJ, P], BF16, tag="q_t")
-            nc.vector.tensor_copy(out=q_t[:], in_=st["pq", h][:])
+            nc.scalar.copy(out=q_t[:], in_=st["pq", h][:])
             st["q_t", h] = q_t
 
         def v_group(h):
             v_g = heads.tile([P, G, D, PACK], BF16, tag="v_g", align_bytes=64)
-            nc.gpsimd.tensor_scalar(
-                out=v_g[:],
-                in0=st["v_sb", h][:].rearrange("p g t d -> p g d t"),
-                scalar1=1.0,
-                scalar2=0.0,
-                op0=ALU.mult,
-                op1=ALU.add,
-            )
+            nc.vector.tensor_copy(out=v_g[:], in_=st["v_sb", h][:].rearrange("p g t d -> p g d t"))
             st["v_g", h] = v_g
 
         def v_quantise(h):
@@ -121,15 +118,19 @@ def tile_scaleddotproductattention_kernel(tc, Q, K, V, mask, out):
             st["mi", j] = mi
 
         def mask_convert(j):
-            mf = mstage.tile([P, G, PACK, P], F32, tag="mf")
-            nc.vector.tensor_scalar(
-                out=mf[:],
-                in0=st["mi", j][:].rearrange("q (g p t w) -> q g t p w", g=G, p=P, t=PACK, w=2)[:, :, :, :, 0],
-                scalar1=MASK_RAW,
-                scalar2=None,
-                op0=ALU.mult,
-            )
-            st["mf", j] = mf
+            words = st["mi", j][:].rearrange("q (g p t w) -> q g t p w", g=G, p=P, t=PACK, w=2)[:, :, :, :, 0]
+            if j in V_MASKED:
+                nc.vector.tensor_scalar(
+                    out=mask_a[:, V_MASKED.index(j), :, :].rearrange("q g (t p) -> q g t p", t=PACK),
+                    in0=words,
+                    scalar1=MASK_SCALED,
+                    scalar2=None,
+                    op0=ALU.mult,
+                )
+            else:
+                mf = mstage.tile([P, G, PACK, P], F32, tag="mf")
+                nc.vector.tensor_scalar(out=mf[:], in0=words, scalar1=MASK_RAW, scalar2=None, op0=ALU.mult)
+                st["mf", j] = mf
 
         def mask_transposes(j, g):
             pm = ps_t.tile([P, PACK, P], F32, tag="tr")
@@ -138,33 +139,54 @@ def tile_scaleddotproductattention_kernel(tc, Q, K, V, mask, out):
             st["pm", j, g] = pm
 
         def mask_copy(j, g):
-            nc.scalar.copy(out=mask_t[:, g * PACK : (g + 1) * PACK, j, :], in_=st["pm", j, g][:])
+            nc.scalar.copy(out=mask_t[:, g * PACK : (g + 1) * PACK, T_MASKED.index(j), :], in_=st["pm", j, g][:])
 
         def scores(i, g):
             h, j = divmod(i, NJ)
             sp = ps_s.tile([P, PACK * P], F32, tag="s")
-            for t in range(PACK):
-                nc.tensor.matmul(
-                    out=sp[:, t * P : (t + 1) * P],
-                    lhsT=mask_t[:, g * PACK + t, j, :],
-                    rhs=ident_f[:],
-                    is_transpose=True,
-                    start=(t == 0),
-                    stop=False,
-                )
+            if j in T_MASKED:
+                for t in range(PACK):
+                    nc.tensor.matmul(
+                        out=sp[:, t * P : (t + 1) * P],
+                        lhsT=mask_t[:, g * PACK + t, T_MASKED.index(j), :],
+                        rhs=ident_f[:],
+                        is_transpose=True,
+                        start=(t == 0),
+                        stop=False,
+                    )
             nc.tensor.matmul(
                 out=sp[:],
                 lhsT=st["q_t", h][:, j, :],
                 rhs=st["k_t", h][:, g * PACK * P : (g + 1) * PACK * P],
-                start=False,
+                start=(j in V_MASKED),
                 stop=True,
             )
             st["sp", i, g] = sp
 
         def row_max(i):
+            j = i % NJ
             neg_s = work.tile([P, G, PACK * P], F32, tag="neg_s")
-            neg_m0 = small.tile([P, 1], F32, tag="neg_m0")
             neg_m = small.tile([P, 1], F32, tag="neg_m")
+            st["neg_s", i] = neg_s
+            st["neg_m", i] = neg_m
+            if j in V_MASKED:
+                for g in range(G):
+                    nc.vector.scalar_tensor_tensor(
+                        out=neg_s[:, g, :],
+                        in0=st["sp", i, g][:],
+                        scalar=-SCALE,
+                        in1=mask_a[:, V_MASKED.index(j), g, :],
+                        op0=ALU.mult,
+                        op1=ALU.add,
+                    )
+                nc.vector.tensor_reduce(
+                    out=neg_m[:],
+                    in_=neg_s[:].rearrange("q g c -> q (g c)"),
+                    axis=mybir.AxisListType.X,
+                    op=ALU.min,
+                )
+                return
+            neg_m0 = small.tile([P, 1], F32, tag="neg_m0")
             nc.vector.tensor_scalar(
                 out=neg_s[:, 0, :],
                 in0=st["sp", i, 0][:],
@@ -183,8 +205,6 @@ def tile_scaleddotproductattention_kernel(tc, Q, K, V, mask, out):
                 op1=ALU.min,
                 accum_out=neg_m[:],
             )
-            st["neg_s", i] = neg_s
-            st["neg_m", i] = neg_m
 
         def exponent(i):
             b, u = divmod(i, UB)
@@ -256,22 +276,26 @@ def tile_scaleddotproductattention_kernel(tc, Q, K, V, mask, out):
                     )
             st["o_ps", b] = o_ps
 
-        def normalise(b):
-            h, half = divmod(b, NJ // UB)
+        def reciprocals(b):
             rinv = batch.tile([P, UB], F32, tag="rinv")
             nc.vector.reciprocal(out=rinv[:], in_=st["rowsum", b][:])
+            st["rinv", b] = rinv
+
+        def normalise(b):
+            h, half = divmod(b, NJ // UB)
             o_sb = batch.tile([P, UB, D], F32, tag="o_sb")
-            nc.vector.tensor_tensor(
-                out=o_sb[:],
-                in0=st["o_ps", b][:],
-                in1=rinv[:].unsqueeze(2).to_broadcast([P, UB, D]),
-                op=ALU.mult,
-            )
+            for u in range(UB):
+                nc.scalar.activation(
+                    out=o_sb[:, u, :],
+                    in_=st["o_ps", b][:, u, :],
+                    func=ACTF.Copy,
+                    scale=st["rinv", b][:, u : u + 1],
+                )
             out_h = out[0, h].rearrange("(p j) d -> p j d", j=NJ)
             nc.sync.dma_start(out=out_h[:, half * UB : (half + 1) * UB, :], in_=o_sb[:])
 
         def prep_step(h):
-            return -2 if h == 0 else (NJ - 1 if h == 1 else NJ * h - 2)
+            return NJ * h - 2
 
         prep_at = dict((prep_step(h), h) for h in range(H))
 
@@ -281,7 +305,7 @@ def tile_scaleddotproductattention_kernel(tc, Q, K, V, mask, out):
         load_v(0)
         mask_load(2)
 
-        for k in range(-2, UNITS + 12):
+        for k in range(-2, UNITS + 13):
             if 3 <= k + 5 < NJ:
                 mask_load(k + 5)
             if k == 3:
@@ -292,11 +316,11 @@ def tile_scaleddotproductattention_kernel(tc, Q, K, V, mask, out):
                 load_v((k - 3) // NJ + 2)
             hp = prep_at.get(k)
             hq = prep_at.get(k - 1)
-            if 0 <= k < NJ:
+            if k in T_MASKED:
                 mask_copy(k, 1)
             if hq is not None:
                 q_copy(hq)
-            if 0 <= k + 1 < NJ:
+            if k + 1 in T_MASKED:
                 mask_transposes(k + 1, 0)
             if hp is not None:
                 k_transposes(hp)
@@ -308,30 +332,32 @@ def tile_scaleddotproductattention_kernel(tc, Q, K, V, mask, out):
                 row_max(k - 1)
             if 0 <= k - 2 < UNITS:
                 exponent(k - 2)
-            if 0 <= k + 1 < NJ:
+            if k + 1 in T_MASKED:
                 mask_copy(k + 1, 0)
             if hp is not None:
                 k_copy(hp)
             if 0 <= k < UNITS:
                 scores(k, 1)
-            if (k - 10) % UB == 0 and 0 <= (k - 10) // UB < BATCHES:
-                pv((k - 10) // UB)
+            if (k - 11) % UB == 0 and 0 <= (k - 11) // UB < BATCHES:
+                pv((k - 11) // UB)
             if 0 <= k - 3 < UNITS:
                 e_transposes(k - 3, GT // 2, GT)
-            if 0 <= k + 1 < NJ:
+            if k + 1 in T_MASKED:
                 mask_transposes(k + 1, 1)
             if hp is not None:
                 q_transposes(hp)
             if 0 <= k - 4 < UNITS:
                 e_copy(k - 4)
+            if (k - 12) % UB == 0 and 0 <= (k - 12) // UB < BATCHES:
+                normalise((k - 12) // UB)
             if 0 <= k - 5 < UNITS:
                 e_group(k - 5)
-            if hp is not None:
-                v_group(hp)
             if (k - 9) % UB == 0 and 0 <= (k - 9) // UB < BATCHES:
                 e_quantise((k - 9) // UB)
-            if (k - 11) % UB == 0 and 0 <= (k - 11) // UB < BATCHES:
-                normalise((k - 11) // UB)
+            if (k - 7) % UB == 0 and 0 <= (k - 7) // UB < BATCHES:
+                reciprocals((k - 7) // UB)
+            if hp is not None:
+                v_group(hp)
             if hq is not None:
                 v_quantise(hq)
             if 0 <= k + 2 < NJ:

@@ -12,6 +12,7 @@ U32 = mybir.dt.uint32
 U8 = mybir.dt.uint8
 ALU = mybir.AluOpType
 ACTF = mybir.ActivationFunctionType
+AX = mybir.AxisListType
 
 P = 128
 H = 16
@@ -28,8 +29,22 @@ SCALE = 1.0 / math.sqrt(D)
 MASK_RAW = -1.0e12 * math.sqrt(D)
 MASK_SCALED = 1.0e12
 FLOPS = 4 * H * N * N * D
-V_MASKED = (1, 3, 5, 7)
-T_MASKED = (0, 2, 4, 6)
+QU = 1
+V_MASKED = (0, 4)
+E_ON_VECTOR = ()
+DIRECT = 4
+NORM_ON_VECTOR = False
+KCOPY_ON_VECTOR = True
+QCOPY_ON_VECTOR = False
+VGROUP_ON_VECTOR = False
+PV_AT = 12
+NORM_AT = 13
+QUANT_AT = 6
+REC_AT = 7
+V0_AT = 4
+PREP_OFF = -2
+PE_ORDER = 0
+T_MASKED = (1, 2, 3, 5, 6, 7)
 
 
 def tile_scaleddotproductattention_kernel(tc, Q, K, V, mask, out):
@@ -52,7 +67,7 @@ def tile_scaleddotproductattention_kernel(tc, Q, K, V, mask, out):
         make_identity(nc, ident_bf[:])
         ident_f = const.tile([P, P], F32)
         make_identity(nc, ident_f[:])
-        mask_t = const.tile([P, GT, NJ - len(V_MASKED), P], F32)
+        mask_t = const.tile([P, GT, len(T_MASKED), P], F32)
         mask_a = const.tile([P, len(V_MASKED), G, PACK * P], BF16)
         mask_words = mask.bitcast(I32).rearrange("(p j) w -> p j w", j=NJ)
 
@@ -81,11 +96,14 @@ def tile_scaleddotproductattention_kernel(tc, Q, K, V, mask, out):
 
         def k_copy(h):
             k_t = heads.tile([P, N], BF16, tag="k_t")
-            nc.scalar.copy(out=k_t[:], in_=st["pk", h][:].rearrange("d c p -> d (c p)"))
+            if KCOPY_ON_VECTOR:
+                nc.vector.tensor_copy(out=k_t[:], in_=st["pk", h][:].rearrange("d c p -> d (c p)"))
+            else:
+                nc.scalar.copy(out=k_t[:], in_=st["pk", h][:].rearrange("d c p -> d (c p)"))
             st["k_t", h] = k_t
 
         def q_transposes(h):
-            pq = ps_t.tile([P, NJ, P], BF16, tag="tr")
+            pq = ps_o.tile([P, NJ, P], BF16, tag="o")
             q_sb = st["q_sb", h]
             for j in range(NJ):
                 nc.tensor.transpose(out=pq[:, j, :], in_=q_sb[:, j, :], identity=ident_bf[:])
@@ -93,12 +111,25 @@ def tile_scaleddotproductattention_kernel(tc, Q, K, V, mask, out):
 
         def q_copy(h):
             q_t = heads.tile([P, NJ, P], BF16, tag="q_t")
-            nc.scalar.copy(out=q_t[:], in_=st["pq", h][:])
+            if QCOPY_ON_VECTOR:
+                nc.vector.tensor_copy(out=q_t[:], in_=st["pq", h][:])
+            else:
+                nc.scalar.copy(out=q_t[:], in_=st["pq", h][:])
             st["q_t", h] = q_t
 
         def v_group(h):
             v_g = heads.tile([P, G, D, PACK], BF16, tag="v_g", align_bytes=64)
-            nc.vector.tensor_copy(out=v_g[:], in_=st["v_sb", h][:].rearrange("p g t d -> p g d t"))
+            if VGROUP_ON_VECTOR:
+                nc.vector.tensor_copy(out=v_g[:], in_=st["v_sb", h][:].rearrange("p g t d -> p g d t"))
+            else:
+                nc.gpsimd.tensor_scalar(
+                    out=v_g[:],
+                    in0=st["v_sb", h][:].rearrange("p g t d -> p g d t"),
+                    scalar1=1.0,
+                    scalar2=0.0,
+                    op0=ALU.mult,
+                    op1=ALU.add,
+                )
             st["v_g", h] = v_g
 
         def v_quantise(h):
@@ -113,7 +144,7 @@ def tile_scaleddotproductattention_kernel(tc, Q, K, V, mask, out):
             st["v_scales", h] = v_scales
 
         def mask_load(j):
-            mi = mstage.tile([P, 2 * N], I32, tag="mi", bufs=4)
+            mi = mstage.tile([P, 2 * N], I32, tag="mi", bufs=NJ)
             nc.sync.dma_start(out=mi[:], in_=mask_words[:, j, :])
             st["mi", j] = mi
 
@@ -141,9 +172,10 @@ def tile_scaleddotproductattention_kernel(tc, Q, K, V, mask, out):
         def mask_copy(j, g):
             nc.scalar.copy(out=mask_t[:, g * PACK : (g + 1) * PACK, T_MASKED.index(j), :], in_=st["pm", j, g][:])
 
-        def scores(i, g):
-            h, j = divmod(i, NJ)
+        def mask_add(i, g):
+            j = i % NJ
             sp = ps_s.tile([P, PACK * P], F32, tag="s")
+            st["sp", i, g] = sp
             if j in T_MASKED:
                 for t in range(PACK):
                     nc.tensor.matmul(
@@ -154,21 +186,23 @@ def tile_scaleddotproductattention_kernel(tc, Q, K, V, mask, out):
                         start=(t == 0),
                         stop=False,
                     )
+
+        def qk(i, g):
+            h, j = divmod(i, NJ)
             nc.tensor.matmul(
-                out=sp[:],
+                out=st["sp", i, g][:],
                 lhsT=st["q_t", h][:, j, :],
                 rhs=st["k_t", h][:, g * PACK * P : (g + 1) * PACK * P],
                 start=(j in V_MASKED),
                 stop=True,
             )
-            st["sp", i, g] = sp
 
         def row_max(i):
             j = i % NJ
             neg_s = work.tile([P, G, PACK * P], F32, tag="neg_s")
-            neg_m = small.tile([P, 1], F32, tag="neg_m")
+            neg_m2 = small.tile([P, G], F32, tag="neg_m2")
             st["neg_s", i] = neg_s
-            st["neg_m", i] = neg_m
+            st["neg_m2", i] = neg_m2
             if j in V_MASKED:
                 for g in range(G):
                     nc.vector.scalar_tensor_tensor(
@@ -179,32 +213,24 @@ def tile_scaleddotproductattention_kernel(tc, Q, K, V, mask, out):
                         op0=ALU.mult,
                         op1=ALU.add,
                     )
-                nc.vector.tensor_reduce(
-                    out=neg_m[:],
-                    in_=neg_s[:].rearrange("q g c -> q (g c)"),
-                    axis=mybir.AxisListType.X,
-                    op=ALU.min,
-                )
-                return
-            neg_m0 = small.tile([P, 1], F32, tag="neg_m0")
-            nc.vector.tensor_scalar(
-                out=neg_s[:, 0, :],
-                in0=st["sp", i, 0][:],
-                scalar1=-SCALE,
-                scalar2=None,
-                op0=ALU.mult,
-                op1=ALU.min,
-                accum_out=neg_m0[:],
-            )
-            nc.vector.tensor_scalar(
-                out=neg_s[:, 1, :],
-                in0=st["sp", i, 1][:],
-                scalar1=-SCALE,
-                scalar2=neg_m0[:, 0:1],
-                op0=ALU.mult,
-                op1=ALU.min,
-                accum_out=neg_m[:],
-            )
+                for g in range(G):
+                    nc.vector.tensor_reduce(out=neg_m2[:, g : g + 1], in_=neg_s[:, g, :], axis=AX.X, op=ALU.min)
+            else:
+                for g in range(G):
+                    nc.vector.tensor_scalar(
+                        out=neg_s[:, g, :],
+                        in0=st["sp", i, g][:],
+                        scalar1=-SCALE,
+                        scalar2=None,
+                        op0=ALU.mult,
+                        op1=ALU.min,
+                        accum_out=neg_m2[:, g : g + 1],
+                    )
+
+        def row_max_join(i):
+            neg_m = small.tile([P, 1], F32, tag="neg_m")
+            nc.vector.tensor_reduce(out=neg_m[:], in_=st["neg_m2", i][:], axis=AX.X, op=ALU.min)
+            st["neg_m", i] = neg_m
 
         def exponent(i):
             b, u = divmod(i, UB)
@@ -231,17 +257,23 @@ def tile_scaleddotproductattention_kernel(tc, Q, K, V, mask, out):
 
         def e_copy(i):
             ec = work.tile([P, GT, P], BF16, tag="ec")
-            nc.scalar.copy(out=ec[:], in_=st["et", i][:])
+            if i % NJ in E_ON_VECTOR:
+                nc.vector.tensor_copy(out=ec[:], in_=st["et", i][:])
+            else:
+                nc.scalar.copy(out=ec[:], in_=st["et", i][:])
             st["ec", i] = ec
 
-        def e_group(i):
-            b, u = divmod(i, UB)
+        def grouped_tile(i):
+            w, u = divmod(i, QU)
             if u == 0:
-                st["grouped", b] = batch.tile(
-                    [P, G, UB * P, PACK], BF16, tag="grouped", name="grouped", align_bytes=64
+                st["grouped", w] = batch.tile(
+                    [P, G, QU * P, PACK], BF16, tag="grouped", name="grouped", align_bytes=64
                 )
+            return st["grouped", w][:, :, u * P : (u + 1) * P, :]
+
+        def e_group(i):
             nc.gpsimd.tensor_scalar(
-                out=st["grouped", b][:, :, u * P : (u + 1) * P, :],
+                out=grouped_tile(i),
                 in0=st["ec", i][:].rearrange("p (g t) q -> p g q t", g=G),
                 scalar1=1.0,
                 scalar2=0.0,
@@ -249,26 +281,32 @@ def tile_scaleddotproductattention_kernel(tc, Q, K, V, mask, out):
                 op1=ALU.add,
             )
 
-        def e_quantise(b):
-            codes = batch.tile([P, G, UB * P], U32, tag="codes", align_bytes=64)
-            scales = batch.tile([P, G, UB * P], U8, tag="scales", align_bytes=64)
+        def e_direct(i):
+            dst = grouped_tile(i)
+            nc.vector.tensor_copy(out=dst[:, 0, :, :], in_=st["et", i][:, 0:PACK, :].rearrange("p t q -> p q t"))
+            nc.scalar.copy(out=dst[:, 1, :, :], in_=st["et", i][:, PACK:GT, :].rearrange("p t q -> p q t"))
+
+        def e_quantise(w):
+            codes = batch.tile([P, G, QU * P], U32, tag="codes", align_bytes=64, bufs=12 // QU)
+            scales = batch.tile([P, G, QU * P], U8, tag="scales", align_bytes=64, bufs=12 // QU)
             nc.vector.quantize_mx(
                 out=codes[:].rearrange("p g q -> p (g q)").bitcast(FP8X4),
                 scales=scales[:].rearrange("p g q -> p (g q)"),
-                in_=st["grouped", b][:].rearrange("p g q t -> p (g q t)"),
+                in_=st["grouped", w][:].rearrange("p g q t -> p (g q t)"),
             )
-            st["codes", b] = codes
-            st["scales", b] = scales
+            st["codes", w] = codes
+            st["scales", w] = scales
 
         def pv(b):
             h = b // (NJ // UB)
             o_ps = ps_o.tile([P, UB, D], F32, tag="o")
             for u in range(UB):
+                w, r = divmod(b * UB + u, QU)
                 for g in range(G):
                     nc.tensor.matmul_mx(
                         out=o_ps[:, u, :],
-                        lhsT=st["codes", b][:, g, u * P : (u + 1) * P].bitcast(FP8X4),
-                        lhsT_scale=st["scales", b][:, g, u * P : (u + 1) * P],
+                        lhsT=st["codes", w][:, g, r * P : (r + 1) * P].bitcast(FP8X4),
+                        lhsT_scale=st["scales", w][:, g, r * P : (r + 1) * P],
                         rhs=st["v_codes", h][:, g * D : (g + 1) * D].bitcast(FP8X4),
                         rhs_scale=st["v_scales", h][:, g * D : (g + 1) * D],
                         start=(g == 0),
@@ -284,50 +322,69 @@ def tile_scaleddotproductattention_kernel(tc, Q, K, V, mask, out):
         def normalise(b):
             h, half = divmod(b, NJ // UB)
             o_sb = batch.tile([P, UB, D], F32, tag="o_sb")
-            for u in range(UB):
-                nc.scalar.activation(
-                    out=o_sb[:, u, :],
-                    in_=st["o_ps", b][:, u, :],
-                    func=ACTF.Copy,
-                    scale=st["rinv", b][:, u : u + 1],
+            if NORM_ON_VECTOR:
+                nc.vector.tensor_tensor(
+                    out=o_sb[:],
+                    in0=st["o_ps", b][:],
+                    in1=st["rinv", b][:].unsqueeze(2).to_broadcast([P, UB, D]),
+                    op=ALU.mult,
                 )
+            else:
+                for u in range(UB):
+                    nc.scalar.activation(
+                        out=o_sb[:, u, :],
+                        in_=st["o_ps", b][:, u, :],
+                        func=ACTF.Copy,
+                        scale=st["rinv", b][:, u : u + 1],
+                    )
             out_h = out[0, h].rearrange("(p j) d -> p j d", j=NJ)
             nc.sync.dma_start(out=out_h[:, half * UB : (half + 1) * UB, :], in_=o_sb[:])
 
-        def prep_step(h):
-            return NJ * h - 2
+        prep_at = dict((-2 if h == 0 else (NJ - 1 if h == 1 else NJ * h + PREP_OFF), h) for h in range(H))
 
-        prep_at = dict((prep_step(h), h) for h in range(H))
+        def due(k, first, every, count):
+            return (k - first) % every == 0 and 0 <= (k - first) // every < count
 
         load_head(0)
-        mask_load(0)
-        mask_load(1)
-        load_v(0)
-        mask_load(2)
+        for j in range(NJ):
+            mask_load(j)
+            if j == 3:
+                load_v(0)
+        load_head(1)
+        load_v(1)
 
-        for k in range(-2, UNITS + 13):
-            if 3 <= k + 5 < NJ:
-                mask_load(k + 5)
-            if k == 3:
-                load_head(1)
-                load_v(1)
+        for k in range(-2, UNITS + 14):
             if k >= 3 and (k - 3) % NJ == 0 and 2 <= (k - 3) // NJ + 2 < H:
                 load_head((k - 3) // NJ + 2)
                 load_v((k - 3) // NJ + 2)
             hp = prep_at.get(k)
             hq = prep_at.get(k - 1)
+            hv = 0 if k == V0_AT else (hp if hp else None)
+            hw = 0 if k == V0_AT + 1 else (hq if hq else None)
+            unit = 0 <= k < UNITS
+            tr_unit = 0 <= k - 3 < UNITS
+            if 0 <= k + 1 < NJ:
+                mask_convert(k + 1)
             if k in T_MASKED:
                 mask_copy(k, 1)
-            if hq is not None:
-                q_copy(hq)
+            if 0 <= k - 2 < UNITS:
+                row_max_join(k - 2)
+            if PE_ORDER == 0:
+                if unit:
+                    mask_add(k, 0)
+                    qk(k, 0)
+                if tr_unit:
+                    e_transposes(k - 3, 0, GT // 2)
+            else:
+                if unit:
+                    mask_add(k, 0)
+                    mask_add(k, 1)
+                    qk(k, 0)
             if k + 1 in T_MASKED:
                 mask_transposes(k + 1, 0)
             if hp is not None:
                 k_transposes(hp)
-            if 0 <= k < UNITS:
-                scores(k, 0)
-            if 0 <= k - 3 < UNITS:
-                e_transposes(k - 3, 0, GT // 2)
+                q_transposes(hp)
             if 0 <= k - 1 < UNITS:
                 row_max(k - 1)
             if 0 <= k - 2 < UNITS:
@@ -336,29 +393,37 @@ def tile_scaleddotproductattention_kernel(tc, Q, K, V, mask, out):
                 mask_copy(k + 1, 0)
             if hp is not None:
                 k_copy(hp)
-            if 0 <= k < UNITS:
-                scores(k, 1)
-            if (k - 11) % UB == 0 and 0 <= (k - 11) // UB < BATCHES:
-                pv((k - 11) // UB)
-            if 0 <= k - 3 < UNITS:
-                e_transposes(k - 3, GT // 2, GT)
+                q_copy(hp)
+            if PE_ORDER == 0:
+                if unit:
+                    mask_add(k, 1)
+                    qk(k, 1)
+                if due(k, PV_AT, UB, BATCHES):
+                    pv((k - PV_AT) // UB)
+                if tr_unit:
+                    e_transposes(k - 3, GT // 2, GT)
+            else:
+                if due(k, PV_AT, UB, BATCHES):
+                    pv((k - PV_AT) // UB)
+                if unit:
+                    qk(k, 1)
+                if tr_unit:
+                    e_transposes(k - 3, 0, GT)
             if k + 1 in T_MASKED:
                 mask_transposes(k + 1, 1)
-            if hp is not None:
-                q_transposes(hp)
-            if 0 <= k - 4 < UNITS:
+            if 0 <= k - 4 < UNITS - DIRECT:
                 e_copy(k - 4)
-            if (k - 12) % UB == 0 and 0 <= (k - 12) // UB < BATCHES:
-                normalise((k - 12) // UB)
-            if 0 <= k - 5 < UNITS:
+            if UNITS - DIRECT <= k - 4 < UNITS:
+                e_direct(k - 4)
+            if due(k, NORM_AT, UB, BATCHES):
+                normalise((k - NORM_AT) // UB)
+            if 0 <= k - 5 < UNITS - DIRECT:
                 e_group(k - 5)
-            if (k - 9) % UB == 0 and 0 <= (k - 9) // UB < BATCHES:
-                e_quantise((k - 9) // UB)
-            if (k - 7) % UB == 0 and 0 <= (k - 7) // UB < BATCHES:
-                reciprocals((k - 7) // UB)
-            if hp is not None:
-                v_group(hp)
-            if hq is not None:
-                v_quantise(hq)
-            if 0 <= k + 2 < NJ:
-                mask_convert(k + 2)
+            if hv is not None:
+                v_group(hv)
+            if due(k, QUANT_AT + QU - 1, QU, UNITS // QU):
+                e_quantise((k - QUANT_AT - (QU - 1)) // QU)
+            if due(k, REC_AT, UB, BATCHES):
+                reciprocals((k - REC_AT) // UB)
+            if hw is not None:
+                v_quantise(hw)

@@ -33,17 +33,21 @@ QU = 1
 V_MASKED = (0, 4)
 E_ON_VECTOR = ()
 DIRECT = 4
-NORM_ON_VECTOR = False
+NORM_ON_VECTOR = True
 KCOPY_ON_VECTOR = True
 QCOPY_ON_VECTOR = False
 VGROUP_ON_VECTOR = False
 PV_AT = 12
-NORM_AT = 13
+NORM_AT = 14
 QUANT_AT = 6
 REC_AT = 7
 V0_AT = 4
-PREP_OFF = -2
-PE_ORDER = 0
+PREP_OFF = -1
+PE_ORDER = 1
+GBUFS = 3
+VPREP_AT = 6
+QUANT_FIRST = False
+EBUFS = 3
 T_MASKED = (1, 2, 3, 5, 6, 7)
 
 
@@ -256,25 +260,28 @@ def tile_scaleddotproductattention_kernel(tc, Q, K, V, mask, out):
                 )
 
         def e_copy(i):
-            ec = work.tile([P, GT, P], BF16, tag="ec")
+            w, u = divmod(i, QU)
+            if u == 0:
+                st["ec", w] = batch.tile([P, GT, QU * P], BF16, tag="ec", name="ec", bufs=EBUFS)
+            dst = st["ec", w][:, :, u * P : (u + 1) * P]
             if i % NJ in E_ON_VECTOR:
-                nc.vector.tensor_copy(out=ec[:], in_=st["et", i][:])
+                nc.vector.tensor_copy(out=dst, in_=st["et", i][:])
             else:
-                nc.scalar.copy(out=ec[:], in_=st["et", i][:])
-            st["ec", i] = ec
+                nc.scalar.copy(out=dst, in_=st["et", i][:])
 
         def grouped_tile(i):
             w, u = divmod(i, QU)
-            if u == 0:
+            if ("grouped", w) not in st:
                 st["grouped", w] = batch.tile(
-                    [P, G, QU * P, PACK], BF16, tag="grouped", name="grouped", align_bytes=64
+                    [P, G, QU * P, PACK], BF16, tag="grouped", name="grouped", align_bytes=64, bufs=GBUFS
                 )
             return st["grouped", w][:, :, u * P : (u + 1) * P, :]
 
-        def e_group(i):
+        def e_group(w):
+            grouped_tile(w * QU)
             nc.gpsimd.tensor_scalar(
-                out=grouped_tile(i),
-                in0=st["ec", i][:].rearrange("p (g t) q -> p g q t", g=G),
+                out=st["grouped", w][:],
+                in0=st["ec", w][:].rearrange("p (g t) x -> p g x t", g=G),
                 scalar1=1.0,
                 scalar2=0.0,
                 op0=ALU.mult,
@@ -345,6 +352,19 @@ def tile_scaleddotproductattention_kernel(tc, Q, K, V, mask, out):
         def due(k, first, every, count):
             return (k - first) % every == 0 and 0 <= (k - first) // every < count
 
+        def quantises(k):
+            if due(k, QUANT_AT + QU - 1, QU, UNITS // QU):
+                e_quantise((k - QUANT_AT - (QU - 1)) // QU)
+            if VGROUP_ON_VECTOR:
+                if due(k, VPREP_AT, NJ, H):
+                    v_group((k - VPREP_AT) // NJ)
+                    v_quantise((k - VPREP_AT) // NJ)
+            else:
+                if due(k, VPREP_AT, NJ, H):
+                    v_group((k - VPREP_AT) // NJ)
+                if due(k, VPREP_AT + 1, NJ, H):
+                    v_quantise((k - VPREP_AT - 1) // NJ)
+
         load_head(0)
         for j in range(NJ):
             mask_load(j)
@@ -359,14 +379,14 @@ def tile_scaleddotproductattention_kernel(tc, Q, K, V, mask, out):
                 load_v((k - 3) // NJ + 2)
             hp = prep_at.get(k)
             hq = prep_at.get(k - 1)
-            hv = 0 if k == V0_AT else (hp if hp else None)
-            hw = 0 if k == V0_AT + 1 else (hq if hq else None)
             unit = 0 <= k < UNITS
             tr_unit = 0 <= k - 3 < UNITS
             if 0 <= k + 1 < NJ:
                 mask_convert(k + 1)
             if k in T_MASKED:
                 mask_copy(k, 1)
+            if QUANT_FIRST:
+                quantises(k)
             if 0 <= k - 2 < UNITS:
                 row_max_join(k - 2)
             if PE_ORDER == 0:
@@ -417,13 +437,9 @@ def tile_scaleddotproductattention_kernel(tc, Q, K, V, mask, out):
                 e_direct(k - 4)
             if due(k, NORM_AT, UB, BATCHES):
                 normalise((k - NORM_AT) // UB)
-            if 0 <= k - 5 < UNITS - DIRECT:
-                e_group(k - 5)
-            if hv is not None:
-                v_group(hv)
-            if due(k, QUANT_AT + QU - 1, QU, UNITS // QU):
-                e_quantise((k - QUANT_AT - (QU - 1)) // QU)
+            if due(k, 5 + QU - 1, QU, (UNITS - DIRECT) // QU):
+                e_group((k - 5 - (QU - 1)) // QU)
+            if not QUANT_FIRST:
+                quantises(k)
             if due(k, REC_AT, UB, BATCHES):
                 reciprocals((k - REC_AT) // UB)
-            if hw is not None:
-                v_quantise(hw)

@@ -21,34 +21,26 @@ D = 128
 NJ = N // P
 PACK = 4
 G = N // (P * PACK)
-GT = G * PACK
+PLANES = G * PACK
+BANK = PACK * P
 UB = 4
 UNITS = H * NJ
 BATCHES = UNITS // UB
 SCALE = 1.0 / math.sqrt(D)
-MASK_RAW = -1.0e12 * math.sqrt(D)
-MASK_SCALED = 1.0e12
+MASKED = -1.0e12 * math.sqrt(D)
 FLOPS = 4 * H * N * N * D
-QU = 1
-V_MASKED = (0, 4)
-E_ON_VECTOR = ()
-DIRECT = 4
-NORM_ON_VECTOR = True
-KCOPY_ON_VECTOR = True
-QCOPY_ON_VECTOR = False
-VGROUP_ON_VECTOR = False
-PV_AT = 12
-NORM_AT = 14
-QUANT_AT = 6
-REC_AT = 7
-V0_AT = 4
-PREP_OFF = -1
-PE_ORDER = 1
-GBUFS = 3
-VPREP_AT = 6
-QUANT_FIRST = False
-EBUFS = 3
-T_MASKED = (1, 2, 3, 5, 6, 7)
+
+LAG_MAX = 1
+LAG_EXP = 2
+LAG_TRANSPOSE = 3
+LAG_COPY = 4
+LAG_GROUP = 5
+LAG_QUANTISE = 6
+LAG_RECIPROCAL = 4
+LAG_PV = 9
+LAG_DIVIDE = 10
+LAST_STEP = UNITS - 1 + LAG_DIVIDE
+CODE_BUFS = UB - 1 + LAG_PV - LAG_QUANTISE + 2
 
 
 def tile_scaleddotproductattention_kernel(tc, Q, K, V, mask, out):
@@ -61,7 +53,7 @@ def tile_scaleddotproductattention_kernel(tc, Q, K, V, mask, out):
         work = ctx.enter_context(tc.tile_pool(name="work", bufs=3))
         small = ctx.enter_context(tc.tile_pool(name="small", bufs=4))
         batch = ctx.enter_context(tc.tile_pool(name="batch", bufs=3))
-        ps_s = ctx.enter_context(tc.psum_pool(name="ps_s", bufs=4))
+        ps_s = ctx.enter_context(tc.psum_pool(name="ps_s", bufs=2 * G))
         ps_e = ctx.enter_context(tc.psum_pool(name="ps_e", bufs=2))
         ps_o = ctx.enter_context(tc.psum_pool(name="ps_o", bufs=1))
         ps_t = ctx.enter_context(tc.psum_pool(name="ps_t", bufs=1))
@@ -71,375 +63,273 @@ def tile_scaleddotproductattention_kernel(tc, Q, K, V, mask, out):
         make_identity(nc, ident_bf[:])
         ident_f = const.tile([P, P], F32)
         make_identity(nc, ident_f[:])
-        mask_t = const.tile([P, GT, len(T_MASKED), P], F32)
-        mask_a = const.tile([P, len(V_MASKED), G, PACK * P], BF16)
+        mask_t = const.tile([P, PLANES, NJ, P], F32)
         mask_words = mask.bitcast(I32).rearrange("(p j) w -> p j w", j=NJ)
 
-        st = {}
+        live = {}
+
 
         def load_head(h):
             k_sb = raw.tile([P, G, PACK, D], BF16, tag="k_sb")
             nc.sync.dma_start(out=k_sb[:], in_=K[0, h].rearrange("(g p t) d -> p g t d", g=G, t=PACK))
             q_sb = raw.tile([P, NJ, D], BF16, tag="q_sb")
             nc.sync.dma_start(out=q_sb[:], in_=Q[0, h].rearrange("(p j) d -> p j d", j=NJ))
-            st["k_sb", h] = k_sb
-            st["q_sb", h] = q_sb
-
-        def load_v(h):
             v_sb = raw.tile([P, G, PACK, D], BF16, tag="v_sb")
             nc.sync.dma_start(out=v_sb[:], in_=V[0, h].rearrange("(g p t) d -> p g t d", g=G, t=PACK))
-            st["v_sb", h] = v_sb
+            live["k_sb", h] = k_sb
+            live["q_sb", h] = q_sb
+            live["v_sb", h] = v_sb
 
-        def k_transposes(h):
-            pk = ps_t.tile([P, GT, P], BF16, tag="tr")
-            k_sb = st["k_sb", h]
+        def transpose_k_and_q(h):
+            pk = ps_t.tile([P, PLANES, P], BF16, tag="tr")
             for g in range(G):
                 for t in range(PACK):
-                    nc.tensor.transpose(out=pk[:, g * PACK + t, :], in_=k_sb[:, g, t, :], identity=ident_bf[:])
-            st["pk", h] = pk
-
-        def k_copy(h):
-            k_t = heads.tile([P, N], BF16, tag="k_t")
-            if KCOPY_ON_VECTOR:
-                nc.vector.tensor_copy(out=k_t[:], in_=st["pk", h][:].rearrange("d c p -> d (c p)"))
-            else:
-                nc.scalar.copy(out=k_t[:], in_=st["pk", h][:].rearrange("d c p -> d (c p)"))
-            st["k_t", h] = k_t
-
-        def q_transposes(h):
+                    nc.tensor.transpose(
+                        out=pk[:, g * PACK + t, :], in_=live["k_sb", h][:, g, t, :], identity=ident_bf[:]
+                    )
             pq = ps_o.tile([P, NJ, P], BF16, tag="o")
-            q_sb = st["q_sb", h]
             for j in range(NJ):
-                nc.tensor.transpose(out=pq[:, j, :], in_=q_sb[:, j, :], identity=ident_bf[:])
-            st["pq", h] = pq
+                nc.tensor.transpose(out=pq[:, j, :], in_=live["q_sb", h][:, j, :], identity=ident_bf[:])
+            live["pk", h] = pk
+            live["pq", h] = pq
 
-        def q_copy(h):
+        def copy_k_and_q(h):
+            k_t = heads.tile([P, N], BF16, tag="k_t")
+            nc.vector.tensor_copy(out=k_t[:], in_=live["pk", h][:].rearrange("d c p -> d (c p)"))
             q_t = heads.tile([P, NJ, P], BF16, tag="q_t")
-            if QCOPY_ON_VECTOR:
-                nc.vector.tensor_copy(out=q_t[:], in_=st["pq", h][:])
-            else:
-                nc.scalar.copy(out=q_t[:], in_=st["pq", h][:])
-            st["q_t", h] = q_t
+            nc.scalar.copy(out=q_t[:], in_=live["pq", h][:])
+            live["k_t", h] = k_t
+            live["q_t", h] = q_t
 
-        def v_group(h):
+        def group_v(h):
             v_g = heads.tile([P, G, D, PACK], BF16, tag="v_g", align_bytes=64)
-            if VGROUP_ON_VECTOR:
-                nc.vector.tensor_copy(out=v_g[:], in_=st["v_sb", h][:].rearrange("p g t d -> p g d t"))
-            else:
-                nc.gpsimd.tensor_scalar(
-                    out=v_g[:],
-                    in0=st["v_sb", h][:].rearrange("p g t d -> p g d t"),
-                    scalar1=1.0,
-                    scalar2=0.0,
-                    op0=ALU.mult,
-                    op1=ALU.add,
-                )
-            st["v_g", h] = v_g
-
-        def v_quantise(h):
-            v_codes = heads.tile([P, G * D], U32, tag="v_codes", align_bytes=64)
-            v_scales = heads.tile([P, G * D], U8, tag="v_scales", align_bytes=64)
-            nc.vector.quantize_mx(
-                out=v_codes[:].bitcast(FP8X4),
-                scales=v_scales[:],
-                in_=st["v_g", h][:].rearrange("p g d t -> p (g d t)"),
-            )
-            st["v_codes", h] = v_codes
-            st["v_scales", h] = v_scales
-
-        def mask_load(j):
-            mi = mstage.tile([P, 2 * N], I32, tag="mi", bufs=NJ)
-            nc.sync.dma_start(out=mi[:], in_=mask_words[:, j, :])
-            st["mi", j] = mi
-
-        def mask_convert(j):
-            words = st["mi", j][:].rearrange("q (g p t w) -> q g t p w", g=G, p=P, t=PACK, w=2)[:, :, :, :, 0]
-            if j in V_MASKED:
-                nc.vector.tensor_scalar(
-                    out=mask_a[:, V_MASKED.index(j), :, :].rearrange("q g (t p) -> q g t p", t=PACK),
-                    in0=words,
-                    scalar1=MASK_SCALED,
-                    scalar2=None,
-                    op0=ALU.mult,
-                )
-            else:
-                mf = mstage.tile([P, G, PACK, P], F32, tag="mf")
-                nc.vector.tensor_scalar(out=mf[:], in0=words, scalar1=MASK_RAW, scalar2=None, op0=ALU.mult)
-                st["mf", j] = mf
-
-        def mask_transposes(j, g):
-            pm = ps_t.tile([P, PACK, P], F32, tag="tr")
-            for t in range(PACK):
-                nc.tensor.transpose(out=pm[:, t, :], in_=st["mf", j][:, g, t, :], identity=ident_f[:])
-            st["pm", j, g] = pm
-
-        def mask_copy(j, g):
-            nc.scalar.copy(out=mask_t[:, g * PACK : (g + 1) * PACK, T_MASKED.index(j), :], in_=st["pm", j, g][:])
-
-        def mask_add(i, g):
-            j = i % NJ
-            sp = ps_s.tile([P, PACK * P], F32, tag="s")
-            st["sp", i, g] = sp
-            if j in T_MASKED:
-                for t in range(PACK):
-                    nc.tensor.matmul(
-                        out=sp[:, t * P : (t + 1) * P],
-                        lhsT=mask_t[:, g * PACK + t, T_MASKED.index(j), :],
-                        rhs=ident_f[:],
-                        is_transpose=True,
-                        start=(t == 0),
-                        stop=False,
-                    )
-
-        def qk(i, g):
-            h, j = divmod(i, NJ)
-            nc.tensor.matmul(
-                out=st["sp", i, g][:],
-                lhsT=st["q_t", h][:, j, :],
-                rhs=st["k_t", h][:, g * PACK * P : (g + 1) * PACK * P],
-                start=(j in V_MASKED),
-                stop=True,
-            )
-
-        def row_max(i):
-            j = i % NJ
-            neg_s = work.tile([P, G, PACK * P], F32, tag="neg_s")
-            neg_m2 = small.tile([P, G], F32, tag="neg_m2")
-            st["neg_s", i] = neg_s
-            st["neg_m2", i] = neg_m2
-            if j in V_MASKED:
-                for g in range(G):
-                    nc.vector.scalar_tensor_tensor(
-                        out=neg_s[:, g, :],
-                        in0=st["sp", i, g][:],
-                        scalar=-SCALE,
-                        in1=mask_a[:, V_MASKED.index(j), g, :],
-                        op0=ALU.mult,
-                        op1=ALU.add,
-                    )
-                for g in range(G):
-                    nc.vector.tensor_reduce(out=neg_m2[:, g : g + 1], in_=neg_s[:, g, :], axis=AX.X, op=ALU.min)
-            else:
-                for g in range(G):
-                    nc.vector.tensor_scalar(
-                        out=neg_s[:, g, :],
-                        in0=st["sp", i, g][:],
-                        scalar1=-SCALE,
-                        scalar2=None,
-                        op0=ALU.mult,
-                        op1=ALU.min,
-                        accum_out=neg_m2[:, g : g + 1],
-                    )
-
-        def row_max_join(i):
-            neg_m = small.tile([P, 1], F32, tag="neg_m")
-            nc.vector.tensor_reduce(out=neg_m[:], in_=st["neg_m2", i][:], axis=AX.X, op=ALU.min)
-            st["neg_m", i] = neg_m
-
-        def exponent(i):
-            b, u = divmod(i, UB)
-            if u == 0:
-                st["rowsum", b] = batch.tile([P, UB], F32, tag="rowsum", name="rowsum", bufs=4)
-            e = work.tile([P, N], BF16, tag="e")
-            nc.scalar.activation(
-                out=e[:],
-                in_=st["neg_s", i][:].rearrange("q g c -> q (g c)"),
-                func=ACTF.Exp,
-                bias=st["neg_m", i][:, 0:1],
-                scale=-1.0,
-                accum_out=st["rowsum", b][:, u : u + 1],
-            )
-            st["e", i] = e
-
-        def e_transposes(i, lo, hi):
-            if lo == 0:
-                st["et", i] = ps_e.tile([P, GT, P], BF16, tag="et", name="et")
-            for c in range(lo, hi):
-                nc.tensor.transpose(
-                    out=st["et", i][:, c, :], in_=st["e", i][:, c * P : (c + 1) * P], identity=ident_bf[:]
-                )
-
-        def e_copy(i):
-            w, u = divmod(i, QU)
-            if u == 0:
-                st["ec", w] = batch.tile([P, GT, QU * P], BF16, tag="ec", name="ec", bufs=EBUFS)
-            dst = st["ec", w][:, :, u * P : (u + 1) * P]
-            if i % NJ in E_ON_VECTOR:
-                nc.vector.tensor_copy(out=dst, in_=st["et", i][:])
-            else:
-                nc.scalar.copy(out=dst, in_=st["et", i][:])
-
-        def grouped_tile(i):
-            w, u = divmod(i, QU)
-            if ("grouped", w) not in st:
-                st["grouped", w] = batch.tile(
-                    [P, G, QU * P, PACK], BF16, tag="grouped", name="grouped", align_bytes=64, bufs=GBUFS
-                )
-            return st["grouped", w][:, :, u * P : (u + 1) * P, :]
-
-        def e_group(w):
-            grouped_tile(w * QU)
             nc.gpsimd.tensor_scalar(
-                out=st["grouped", w][:],
-                in0=st["ec", w][:].rearrange("p (g t) x -> p g x t", g=G),
+                out=v_g[:],
+                in0=live["v_sb", h][:].rearrange("p g t d -> p g d t"),
                 scalar1=1.0,
                 scalar2=0.0,
                 op0=ALU.mult,
                 op1=ALU.add,
             )
+            live["v_g", h] = v_g
 
-        def e_direct(i):
-            dst = grouped_tile(i)
-            nc.vector.tensor_copy(out=dst[:, 0, :, :], in_=st["et", i][:, 0:PACK, :].rearrange("p t q -> p q t"))
-            nc.scalar.copy(out=dst[:, 1, :, :], in_=st["et", i][:, PACK:GT, :].rearrange("p t q -> p q t"))
+        def quantise_v(h):
+            v_codes = heads.tile([P, G * D], U32, tag="v_codes", align_bytes=64)
+            v_scales = heads.tile([P, G * D], U8, tag="v_scales", align_bytes=64)
+            nc.vector.quantize_mx(
+                out=v_codes[:].bitcast(FP8X4),
+                scales=v_scales[:],
+                in_=live["v_g", h][:].rearrange("p g d t -> p (g d t)"),
+            )
+            live["v_codes", h] = v_codes
+            live["v_scales", h] = v_scales
 
-        def e_quantise(w):
-            codes = batch.tile([P, G, QU * P], U32, tag="codes", align_bytes=64, bufs=12 // QU)
-            scales = batch.tile([P, G, QU * P], U8, tag="scales", align_bytes=64, bufs=12 // QU)
+
+        def load_mask(j):
+            mi = mstage.tile([P, 2 * N], I32, tag="mi", bufs=NJ)
+            nc.sync.dma_start(out=mi[:], in_=mask_words[:, j, :])
+            live["mi", j] = mi
+
+        def convert_mask(j):
+            mf = mstage.tile([P, G, PACK, P], F32, tag="mf")
+            nc.vector.tensor_scalar(
+                out=mf[:],
+                in0=live["mi", j][:].rearrange("q (g p t w) -> q g t p w", g=G, p=P, t=PACK, w=2)[:, :, :, :, 0],
+                scalar1=MASKED,
+                scalar2=None,
+                op0=ALU.mult,
+            )
+            live["mf", j] = mf
+
+        def transpose_mask(j, g):
+            pm = ps_t.tile([P, PACK, P], F32, tag="tr")
+            for t in range(PACK):
+                nc.tensor.transpose(out=pm[:, t, :], in_=live["mf", j][:, g, t, :], identity=ident_f[:])
+            live["pm", j, g] = pm
+
+        def copy_mask(j, g):
+            nc.scalar.copy(out=mask_t[:, g * PACK : (g + 1) * PACK, j, :], in_=live["pm", j, g][:])
+
+
+        def scores(i, g):
+            h, j = divmod(i, NJ)
+            sp = ps_s.tile([P, BANK], F32, tag="s")
+            for t in range(PACK):
+                nc.tensor.matmul(
+                    out=sp[:, t * P : (t + 1) * P],
+                    lhsT=mask_t[:, g * PACK + t, j, :],
+                    rhs=ident_f[:],
+                    is_transpose=True,
+                    start=(t == 0),
+                    stop=False,
+                )
+            nc.tensor.matmul(
+                out=sp[:],
+                lhsT=live["q_t", h][:, j, :],
+                rhs=live["k_t", h][:, g * BANK : (g + 1) * BANK],
+                start=False,
+                stop=True,
+            )
+            live["sp", i, g] = sp
+
+        def row_max(i):
+            neg_s = work.tile([P, G, BANK], F32, tag="neg_s")
+            neg_m2 = small.tile([P, G], F32, tag="neg_m2")
+            for g in range(G):
+                nc.vector.tensor_scalar(
+                    out=neg_s[:, g, :],
+                    in0=live["sp", i, g][:],
+                    scalar1=-SCALE,
+                    scalar2=None,
+                    op0=ALU.mult,
+                    op1=ALU.min,
+                    accum_out=neg_m2[:, g : g + 1],
+                )
+            live["neg_s", i] = neg_s
+            live["neg_m2", i] = neg_m2
+
+        def join_row_max(i):
+            neg_m = small.tile([P, 1], F32, tag="neg_m")
+            nc.vector.tensor_reduce(out=neg_m[:], in_=live["neg_m2", i][:], axis=AX.X, op=ALU.min)
+            live["neg_m", i] = neg_m
+
+        def exponent(i):
+            b, u = divmod(i, UB)
+            if u == 0:
+                live["rowsum", b] = batch.tile([P, UB], F32, tag="rowsum", name="rowsum", bufs=4)
+            e = work.tile([P, N], BF16, tag="e")
+            nc.scalar.activation(
+                out=e[:],
+                in_=live["neg_s", i][:].rearrange("q g c -> q (g c)"),
+                func=ACTF.Exp,
+                bias=live["neg_m", i][:, 0:1],
+                scale=-1.0,
+                accum_out=live["rowsum", b][:, u : u + 1],
+            )
+            live["e", i] = e
+
+        def transpose_e(i, planes):
+            if ("et", i) not in live:
+                live["et", i] = ps_e.tile([P, PLANES, P], BF16, tag="et", name="et")
+            for c in planes:
+                nc.tensor.transpose(
+                    out=live["et", i][:, c, :], in_=live["e", i][:, c * P : (c + 1) * P], identity=ident_bf[:]
+                )
+
+        def copy_e(i):
+            ec = work.tile([P, PLANES, P], BF16, tag="ec")
+            nc.scalar.copy(out=ec[:], in_=live["et", i][:])
+            live["ec", i] = ec
+
+        def group_e(i):
+            grouped = batch.tile([P, G, P, PACK], BF16, tag="grouped", align_bytes=64)
+            nc.gpsimd.tensor_scalar(
+                out=grouped[:],
+                in0=live["ec", i][:].rearrange("p (g t) q -> p g q t", g=G),
+                scalar1=1.0,
+                scalar2=0.0,
+                op0=ALU.mult,
+                op1=ALU.add,
+            )
+            live["grouped", i] = grouped
+
+        def quantise_e(i):
+            codes = batch.tile([P, G, P], U32, tag="codes", align_bytes=64, bufs=CODE_BUFS)
+            scales = batch.tile([P, G, P], U8, tag="scales", align_bytes=64, bufs=CODE_BUFS)
             nc.vector.quantize_mx(
                 out=codes[:].rearrange("p g q -> p (g q)").bitcast(FP8X4),
                 scales=scales[:].rearrange("p g q -> p (g q)"),
-                in_=st["grouped", w][:].rearrange("p g q t -> p (g q t)"),
+                in_=live["grouped", i][:].rearrange("p g q t -> p (g q t)"),
             )
-            st["codes", w] = codes
-            st["scales", w] = scales
+            live["codes", i] = codes
+            live["scales", i] = scales
 
-        def pv(b):
-            h = b // (NJ // UB)
-            o_ps = ps_o.tile([P, UB, D], F32, tag="o")
-            for u in range(UB):
-                w, r = divmod(b * UB + u, QU)
-                for g in range(G):
-                    nc.tensor.matmul_mx(
-                        out=o_ps[:, u, :],
-                        lhsT=st["codes", w][:, g, r * P : (r + 1) * P].bitcast(FP8X4),
-                        lhsT_scale=st["scales", w][:, g, r * P : (r + 1) * P],
-                        rhs=st["v_codes", h][:, g * D : (g + 1) * D].bitcast(FP8X4),
-                        rhs_scale=st["v_scales", h][:, g * D : (g + 1) * D],
-                        start=(g == 0),
-                        stop=(g == G - 1),
-                    )
-            st["o_ps", b] = o_ps
 
         def reciprocals(b):
             rinv = batch.tile([P, UB], F32, tag="rinv")
-            nc.vector.reciprocal(out=rinv[:], in_=st["rowsum", b][:])
-            st["rinv", b] = rinv
+            nc.vector.reciprocal(out=rinv[:], in_=live["rowsum", b][:])
+            live["rinv", b] = rinv
 
-        def normalise(b):
-            h, half = divmod(b, NJ // UB)
-            o_sb = batch.tile([P, UB, D], F32, tag="o_sb")
-            if NORM_ON_VECTOR:
-                nc.vector.tensor_tensor(
-                    out=o_sb[:],
-                    in0=st["o_ps", b][:],
-                    in1=st["rinv", b][:].unsqueeze(2).to_broadcast([P, UB, D]),
-                    op=ALU.mult,
-                )
-            else:
-                for u in range(UB):
-                    nc.scalar.activation(
-                        out=o_sb[:, u, :],
-                        in_=st["o_ps", b][:, u, :],
-                        func=ACTF.Copy,
-                        scale=st["rinv", b][:, u : u + 1],
+        def e_times_v(b):
+            h = b * UB // NJ
+            o_ps = ps_o.tile([P, UB, D], F32, tag="o")
+            for u in range(UB):
+                for g in range(G):
+                    nc.tensor.matmul_mx(
+                        out=o_ps[:, u, :],
+                        lhsT=live["codes", b * UB + u][:, g, :].bitcast(FP8X4),
+                        lhsT_scale=live["scales", b * UB + u][:, g, :],
+                        rhs=live["v_codes", h][:, g * D : (g + 1) * D].bitcast(FP8X4),
+                        rhs_scale=live["v_scales", h][:, g * D : (g + 1) * D],
+                        start=(g == 0),
+                        stop=(g == G - 1),
                     )
-            out_h = out[0, h].rearrange("(p j) d -> p j d", j=NJ)
-            nc.sync.dma_start(out=out_h[:, half * UB : (half + 1) * UB, :], in_=o_sb[:])
+            live["o_ps", b] = o_ps
 
-        prep_at = dict((-2 if h == 0 else (NJ - 1 if h == 1 else NJ * h + PREP_OFF), h) for h in range(H))
+        def divide_and_store(b):
+            h, j0 = divmod(b * UB, NJ)
+            o_sb = batch.tile([P, UB, D], F32, tag="o_sb")
+            for u in range(UB):
+                nc.scalar.activation(
+                    out=o_sb[:, u, :],
+                    in_=live["o_ps", b][:, u, :],
+                    func=ACTF.Copy,
+                    scale=live["rinv", b][:, u : u + 1],
+                )
+            nc.sync.dma_start(out=out[0, h].rearrange("(p j) d -> p j d", j=NJ)[:, j0 : j0 + UB, :], in_=o_sb[:])
 
-        def due(k, first, every, count):
-            return (k - first) % every == 0 and 0 <= (k - first) // every < count
 
-        def quantises(k):
-            if due(k, QUANT_AT + QU - 1, QU, UNITS // QU):
-                e_quantise((k - QUANT_AT - (QU - 1)) // QU)
-            if VGROUP_ON_VECTOR:
-                if due(k, VPREP_AT, NJ, H):
-                    v_group((k - VPREP_AT) // NJ)
-                    v_quantise((k - VPREP_AT) // NJ)
-            else:
-                if due(k, VPREP_AT, NJ, H):
-                    v_group((k - VPREP_AT) // NJ)
-                if due(k, VPREP_AT + 1, NJ, H):
-                    v_quantise((k - VPREP_AT - 1) // NJ)
+        def unit_at(k, lag):
+            return k - lag if 0 <= k - lag < UNITS else None
+
+        def batch_at(k, lag):
+            b, u = divmod(k - lag, UB)
+            return b if u == UB - 1 and 0 <= b < BATCHES else None
+
+        def head_at(k, lead):
+            h, j = divmod(k + lead, NJ)
+            return h if j == 0 and 0 <= h < H else None
+
+        def mask_tile_at(k, lead):
+            return k + lead if 0 <= k + lead < NJ else None
+
+        def head_to_transpose(k):
+            if k == NJ - 1:
+                return 1
+            h = head_at(k, 2)
+            return None if h == 1 else h
+
+        def run(stage, index, *more):
+            if index is not None:
+                stage(index, *more)
+
 
         load_head(0)
         for j in range(NJ):
-            mask_load(j)
-            if j == 3:
-                load_v(0)
+            load_mask(j)
         load_head(1)
-        load_v(1)
 
-        for k in range(-2, UNITS + 14):
-            if k >= 3 and (k - 3) % NJ == 0 and 2 <= (k - 3) // NJ + 2 < H:
-                load_head((k - 3) // NJ + 2)
-                load_v((k - 3) // NJ + 2)
-            hp = prep_at.get(k)
-            hq = prep_at.get(k - 1)
-            unit = 0 <= k < UNITS
-            tr_unit = 0 <= k - 3 < UNITS
-            if 0 <= k + 1 < NJ:
-                mask_convert(k + 1)
-            if k in T_MASKED:
-                mask_copy(k, 1)
-            if QUANT_FIRST:
-                quantises(k)
-            if 0 <= k - 2 < UNITS:
-                row_max_join(k - 2)
-            if PE_ORDER == 0:
-                if unit:
-                    mask_add(k, 0)
-                    qk(k, 0)
-                if tr_unit:
-                    e_transposes(k - 3, 0, GT // 2)
-            else:
-                if unit:
-                    mask_add(k, 0)
-                    mask_add(k, 1)
-                    qk(k, 0)
-            if k + 1 in T_MASKED:
-                mask_transposes(k + 1, 0)
-            if hp is not None:
-                k_transposes(hp)
-                q_transposes(hp)
-            if 0 <= k - 1 < UNITS:
-                row_max(k - 1)
-            if 0 <= k - 2 < UNITS:
-                exponent(k - 2)
-            if k + 1 in T_MASKED:
-                mask_copy(k + 1, 0)
-            if hp is not None:
-                k_copy(hp)
-                q_copy(hp)
-            if PE_ORDER == 0:
-                if unit:
-                    mask_add(k, 1)
-                    qk(k, 1)
-                if due(k, PV_AT, UB, BATCHES):
-                    pv((k - PV_AT) // UB)
-                if tr_unit:
-                    e_transposes(k - 3, GT // 2, GT)
-            else:
-                if due(k, PV_AT, UB, BATCHES):
-                    pv((k - PV_AT) // UB)
-                if unit:
-                    qk(k, 1)
-                if tr_unit:
-                    e_transposes(k - 3, 0, GT)
-            if k + 1 in T_MASKED:
-                mask_transposes(k + 1, 1)
-            if 0 <= k - 4 < UNITS - DIRECT:
-                e_copy(k - 4)
-            if UNITS - DIRECT <= k - 4 < UNITS:
-                e_direct(k - 4)
-            if due(k, NORM_AT, UB, BATCHES):
-                normalise((k - NORM_AT) // UB)
-            if due(k, 5 + QU - 1, QU, (UNITS - DIRECT) // QU):
-                e_group((k - 5 - (QU - 1)) // QU)
-            if not QUANT_FIRST:
-                quantises(k)
-            if due(k, REC_AT, UB, BATCHES):
-                reciprocals((k - REC_AT) // UB)
+        for k in range(-2, LAST_STEP + 1):
+            run(load_head, head_at(k, 13))
+            run(convert_mask, mask_tile_at(k, 1))
+            run(copy_mask, mask_tile_at(k, 0), 1)
+            run(join_row_max, unit_at(k, LAG_EXP))
+            run(scores, unit_at(k, 0), 0)
+            run(transpose_e, unit_at(k, LAG_TRANSPOSE), range(0, PACK))
+            run(transpose_mask, mask_tile_at(k, 1), 0)
+            run(transpose_k_and_q, head_to_transpose(k))
+            run(row_max, unit_at(k, LAG_MAX))
+            run(exponent, unit_at(k, LAG_EXP))
+            run(copy_mask, mask_tile_at(k, 1), 0)
+            run(copy_k_and_q, head_to_transpose(k))
+            run(scores, unit_at(k, 0), 1)
+            run(e_times_v, batch_at(k, LAG_PV))
+            run(transpose_e, unit_at(k, LAG_TRANSPOSE), range(PACK, PLANES))
+            run(transpose_mask, mask_tile_at(k, 1), 1)
+            run(copy_e, unit_at(k, LAG_COPY))
+            run(divide_and_store, batch_at(k, LAG_DIVIDE))
+            run(group_e, unit_at(k, LAG_GROUP))
+            run(group_v, head_at(k, -4))
+            run(quantise_e, unit_at(k, LAG_QUANTISE))
+            run(reciprocals, batch_at(k, LAG_RECIPROCAL))
+            run(quantise_v, head_at(k, -5))

@@ -22,6 +22,8 @@ NJ = N // P
 PACK = 4
 G = N // (P * PACK)
 PLANES = G * PACK
+PAIR = 2
+WB = PLANES // PAIR
 BANK = PACK * P
 UB = 4
 UNITS = H * NJ
@@ -34,11 +36,10 @@ LAG_MAX = 1
 LAG_EXP = 2
 LAG_TRANSPOSE = 3
 LAG_COPY = 4
-LAG_GROUP = 5
-LAG_QUANTISE = 6
+LAG_QUANTISE = 5
 LAG_RECIPROCAL = 4
-LAG_PV = 9
-LAG_DIVIDE = 10
+LAG_PV = 8
+LAG_DIVIDE = 9
 LAST_STEP = UNITS - 1 + LAG_DIVIDE
 CODE_BUFS = UB - 1 + LAG_PV - LAG_QUANTISE + 2
 
@@ -95,7 +96,10 @@ def tile_scaleddotproductattention_kernel(tc, Q, K, V, mask, out):
 
         def copy_k_and_q(h):
             k_t = heads.tile([P, N], BF16, tag="k_t")
-            nc.vector.tensor_copy(out=k_t[:], in_=live["pk", h][:].rearrange("d c p -> d (c p)"))
+            nc.vector.tensor_copy(
+                out=k_t[:].rearrange("d (a p e) -> d a p e", a=WB, e=PAIR),
+                in_=live["pk", h][:].rearrange("d (a e) p -> d a p e", e=PAIR),
+            )
             q_t = heads.tile([P, NJ, P], BF16, tag="q_t")
             nc.scalar.copy(out=q_t[:], in_=live["pq", h][:])
             live["k_t", h] = k_t
@@ -132,13 +136,15 @@ def tile_scaleddotproductattention_kernel(tc, Q, K, V, mask, out):
 
         def convert_mask(j):
             mf = mstage.tile([P, G, PACK, P], F32, tag="mf")
-            nc.vector.tensor_scalar(
-                out=mf[:],
-                in0=live["mi", j][:].rearrange("q (g p t w) -> q g t p w", g=G, p=P, t=PACK, w=2)[:, :, :, :, 0],
-                scalar1=MASKED,
-                scalar2=None,
-                op0=ALU.mult,
-            )
+            words = live["mi", j][:].rearrange("q (g p u e w) -> q g u p e w", g=G, p=P, u=PAIR, e=PAIR, w=2)
+            for g in range(G):
+                nc.vector.tensor_scalar(
+                    out=mf[:, g].rearrange("q r c -> q (r c)").rearrange("q (u p e) -> q u p e", u=PAIR, e=PAIR),
+                    in0=words[:, g, :, :, :, 0],
+                    scalar1=MASKED,
+                    scalar2=None,
+                    op0=ALU.mult,
+                )
             live["mf", j] = mf
 
         def transpose_mask(j, g):
@@ -208,28 +214,21 @@ def tile_scaleddotproductattention_kernel(tc, Q, K, V, mask, out):
             )
             live["e", i] = e
 
-        def transpose_e(i, planes):
+        def transpose_e(i, blocks):
             if ("et", i) not in live:
-                live["et", i] = ps_e.tile([P, PLANES, P], BF16, tag="et", name="et")
-            for c in planes:
-                nc.tensor.transpose(
-                    out=live["et", i][:, c, :], in_=live["e", i][:, c * P : (c + 1) * P], identity=ident_bf[:]
-                )
+                live["et", i] = ps_e.tile([P, WB, P], F32, tag="et", name="et")
+            e_words = live["e", i][:].bitcast(F32)
+            for a in blocks:
+                nc.tensor.transpose(out=live["et", i][:, a, :], in_=e_words[:, a * P : (a + 1) * P], identity=ident_f[:])
 
         def copy_e(i):
-            ec = work.tile([P, PLANES, P], BF16, tag="ec")
-            nc.scalar.copy(out=ec[:], in_=live["et", i][:])
-            live["ec", i] = ec
-
-        def group_e(i):
             grouped = batch.tile([P, G, P, PACK], BF16, tag="grouped", align_bytes=64)
-            nc.gpsimd.tensor_scalar(
-                out=grouped[:],
-                in0=live["ec", i][:].rearrange("p (g t) q -> p g q t", g=G),
-                scalar1=1.0,
-                scalar2=0.0,
-                op0=ALU.mult,
-                op1=ALU.add,
+            nc.scalar.copy(
+                out=grouped[:]
+                .rearrange("p g q t -> p (g q t)")
+                .bitcast(F32)
+                .rearrange("p (g q u) -> p g q u", g=G, u=PAIR),
+                in_=live["et", i][:].rearrange("p (g u) q -> p g q u", u=PAIR),
             )
             live["grouped", i] = grouped
 
@@ -315,7 +314,7 @@ def tile_scaleddotproductattention_kernel(tc, Q, K, V, mask, out):
             run(copy_mask, mask_tile_at(k, 0), 1)
             run(join_row_max, unit_at(k, LAG_EXP))
             run(scores, unit_at(k, 0), 0)
-            run(transpose_e, unit_at(k, LAG_TRANSPOSE), range(0, PACK))
+            run(transpose_e, unit_at(k, LAG_TRANSPOSE), range(0, PAIR))
             run(transpose_mask, mask_tile_at(k, 1), 0)
             run(transpose_k_and_q, head_to_transpose(k))
             run(row_max, unit_at(k, LAG_MAX))
@@ -324,11 +323,10 @@ def tile_scaleddotproductattention_kernel(tc, Q, K, V, mask, out):
             run(copy_k_and_q, head_to_transpose(k))
             run(scores, unit_at(k, 0), 1)
             run(e_times_v, batch_at(k, LAG_PV))
-            run(transpose_e, unit_at(k, LAG_TRANSPOSE), range(PACK, PLANES))
+            run(transpose_e, unit_at(k, LAG_TRANSPOSE), range(PAIR, WB))
             run(transpose_mask, mask_tile_at(k, 1), 1)
             run(copy_e, unit_at(k, LAG_COPY))
             run(divide_and_store, batch_at(k, LAG_DIVIDE))
-            run(group_e, unit_at(k, LAG_GROUP))
             run(group_v, head_at(k, -4))
             run(quantise_e, unit_at(k, LAG_QUANTISE))
             run(reciprocals, batch_at(k, LAG_RECIPROCAL))

@@ -268,13 +268,12 @@ def tile_scaleddotproductattention_kernel(tc, Q, K, V, mask, out):
         def divide_and_store(b):
             h, j0 = divmod(b * UB, NJ)
             o_sb = batch.tile([P, UB, D], F32, tag="o_sb")
-            for u in range(UB):
-                nc.scalar.activation(
-                    out=o_sb[:, u, :],
-                    in_=live["o_ps", b][:, u, :],
-                    func=ACTF.Copy,
-                    scale=live["rinv", b][:, u : u + 1],
-                )
+            nc.vector.tensor_tensor(
+                out=o_sb[:],
+                in0=live["o_ps", b][:],
+                in1=live["rinv", b][:].unsqueeze(2).to_broadcast([P, UB, D]),
+                op=ALU.mult,
+            )
             nc.sync.dma_start(out=out[0, h].rearrange("(p j) d -> p j d", j=NJ)[:, j0 : j0 + UB, :], in_=o_sb[:])
 
 
@@ -326,8 +325,8 @@ def tile_scaleddotproductattention_kernel(tc, Q, K, V, mask, out):
             run(transpose_e, unit_at(k, LAG_TRANSPOSE), range(PAIR, WB))
             run(transpose_mask, mask_tile_at(k, 1), 1)
             run(copy_e, unit_at(k, LAG_COPY))
-            run(divide_and_store, batch_at(k, LAG_DIVIDE))
             run(group_v, head_at(k, -4))
             run(quantise_e, unit_at(k, LAG_QUANTISE))
+            run(divide_and_store, batch_at(k, LAG_DIVIDE))
             run(reciprocals, batch_at(k, LAG_RECIPROCAL))
             run(quantise_v, head_at(k, -5))

@@ -12,7 +12,6 @@ U32 = mybir.dt.uint32
 U8 = mybir.dt.uint8
 ALU = mybir.AluOpType
 ACTF = mybir.ActivationFunctionType
-AX = mybir.AxisListType
 
 P = 128
 H = 16
@@ -196,7 +195,14 @@ def tile_scaleddotproductattention_kernel(tc, Q, K, V, mask, out):
 
         def join_row_max(i):
             neg_m = small.tile([P, 1], F32, tag="neg_m")
-            nc.vector.tensor_reduce(out=neg_m[:], in_=live["neg_m2", i][:], axis=AX.X, op=ALU.min)
+            nc.gpsimd.tensor_scalar(
+                out=neg_m[:],
+                in0=live["neg_m2", i][:, 0:1],
+                scalar1=live["neg_m2", i][:, 1:2],
+                scalar2=-3.0e38,
+                op0=ALU.min,
+                op1=ALU.max,
+            )
             live["neg_m", i] = neg_m
 
         def exponent(i):
@@ -311,12 +317,12 @@ def tile_scaleddotproductattention_kernel(tc, Q, K, V, mask, out):
             run(load_head, head_at(k, 13))
             run(convert_mask, mask_tile_at(k, 1))
             run(copy_mask, mask_tile_at(k, 0), 1)
-            run(join_row_max, unit_at(k, LAG_EXP))
             run(scores, unit_at(k, 0), 0)
             run(transpose_e, unit_at(k, LAG_TRANSPOSE), range(0, PAIR))
             run(transpose_mask, mask_tile_at(k, 1), 0)
             run(transpose_k_and_q, head_to_transpose(k))
             run(row_max, unit_at(k, LAG_MAX))
+            run(join_row_max, unit_at(k, LAG_MAX))
             run(exponent, unit_at(k, LAG_EXP))
             run(copy_mask, mask_tile_at(k, 1), 0)
             run(copy_k_and_q, head_to_transpose(k))

@@ -146,17 +146,21 @@ def tile_scaleddotproductattention_kernel(tc, Q, K, V, mask, out):
                 )
             live["mf", j] = mf
 
-        def transpose_mask(j, g):
-            pm = ps_t.tile([P, PACK, P], F32, tag="tr")
-            for t in range(PACK):
-                nc.tensor.transpose(out=pm[:, t, :], in_=live["mf", j][:, g, t, :], identity=ident_f[:])
-            live["pm", j, g] = pm
+        def transpose_mask(j):
+            live["pm", j, 0] = ps_t.tile([P, PACK, P], F32, tag="tr", name="pm0")
+            live["pm", j, 1] = ps_o.tile([P, PACK, P], F32, tag="o", name="pm1")
+            for g in range(G):
+                for t in range(PACK):
+                    nc.tensor.transpose(
+                        out=live["pm", j, g][:, t, :], in_=live["mf", j][:, g, t, :], identity=ident_f[:]
+                    )
 
-        def copy_mask(j, g):
-            nc.scalar.copy(out=mask_t[:, g * PACK : (g + 1) * PACK, j, :], in_=live["pm", j, g][:])
+        def copy_mask(j):
+            for g in range(G):
+                nc.scalar.copy(out=mask_t[:, g * PACK : (g + 1) * PACK, j, :], in_=live["pm", j, g][:])
 
 
-        def scores(i, g):
+        def mask_scores(i, g):
             h, j = divmod(i, NJ)
             sp = ps_s.tile([P, BANK], F32, tag="s")
             for t in range(PACK):
@@ -168,14 +172,17 @@ def tile_scaleddotproductattention_kernel(tc, Q, K, V, mask, out):
                     start=(t == 0),
                     stop=False,
                 )
+            live["sp", i, g] = sp
+
+        def q_times_k(i, g):
+            h, j = divmod(i, NJ)
             nc.tensor.matmul(
-                out=sp[:],
+                out=live["sp", i, g][:],
                 lhsT=live["q_t", h][:, j, :],
                 rhs=live["k_t", h][:, g * BANK : (g + 1) * BANK],
                 start=False,
                 stop=True,
             )
-            live["sp", i, g] = sp
 
         def row_max(i):
             neg_s = work.tile([P, G, BANK], F32, tag="neg_s")
@@ -298,9 +305,9 @@ def tile_scaleddotproductattention_kernel(tc, Q, K, V, mask, out):
             return k + lead if 0 <= k + lead < NJ else None
 
         def head_to_transpose(k):
-            if k == NJ - 1:
+            if k == NJ - 2:
                 return 1
-            h = head_at(k, 2)
+            h = head_at(k, 3)
             return None if h == 1 else h
 
         def run(stage, index, *more):
@@ -313,23 +320,22 @@ def tile_scaleddotproductattention_kernel(tc, Q, K, V, mask, out):
             load_mask(j)
         load_head(1)
 
-        for k in range(-2, LAST_STEP + 1):
+        for k in range(-3, LAST_STEP + 1):
             run(load_head, head_at(k, 13))
-            run(convert_mask, mask_tile_at(k, 1))
-            run(copy_mask, mask_tile_at(k, 0), 1)
-            run(scores, unit_at(k, 0), 0)
-            run(transpose_e, unit_at(k, LAG_TRANSPOSE), range(0, PAIR))
-            run(transpose_mask, mask_tile_at(k, 1), 0)
+            run(copy_k_and_q, head_to_transpose(k - 1))
+            run(transpose_mask, mask_tile_at(k, 1))
+            run(copy_mask, mask_tile_at(k, 1))
+            run(mask_scores, unit_at(k, 0), 0)
+            run(mask_scores, unit_at(k, 0), 1)
+            run(q_times_k, unit_at(k, 0), 0)
+            run(e_times_v, batch_at(k, LAG_PV))
+            run(q_times_k, unit_at(k, 0), 1)
+            run(transpose_e, unit_at(k, LAG_TRANSPOSE), range(WB))
             run(transpose_k_and_q, head_to_transpose(k))
+            run(convert_mask, mask_tile_at(k, 2))
             run(row_max, unit_at(k, LAG_MAX))
             run(join_row_max, unit_at(k, LAG_MAX))
             run(exponent, unit_at(k, LAG_EXP))
-            run(copy_mask, mask_tile_at(k, 1), 0)
-            run(copy_k_and_q, head_to_transpose(k))
-            run(scores, unit_at(k, 0), 1)
-            run(e_times_v, batch_at(k, LAG_PV))
-            run(transpose_e, unit_at(k, LAG_TRANSPOSE), range(PAIR, WB))
-            run(transpose_mask, mask_tile_at(k, 1), 1)
             run(copy_e, unit_at(k, LAG_COPY))
             run(group_v, head_at(k, -4))
             run(quantise_e, unit_at(k, LAG_QUANTISE))

@@ -32,10 +32,10 @@ MASKED = -1.0e12 * math.sqrt(D)
 FLOPS = 4 * H * N * N * D
 
 LAG_MAX = 1
-LAG_EXP = 2
-LAG_TRANSPOSE = 3
-LAG_COPY = 4
-LAG_QUANTISE = 5
+LAG_EXP = 3
+LAG_TRANSPOSE = 4
+LAG_COPY = 5
+LAG_QUANTISE = 7
 LAG_RECIPROCAL = 4
 LAG_PV = 8
 LAG_DIVIDE = 9
@@ -50,8 +50,8 @@ def tile_scaleddotproductattention_kernel(tc, Q, K, V, mask, out):
         mstage = ctx.enter_context(tc.tile_pool(name="mstage", bufs=2))
         raw = ctx.enter_context(tc.tile_pool(name="raw", bufs=3))
         heads = ctx.enter_context(tc.tile_pool(name="heads", bufs=3))
-        work = ctx.enter_context(tc.tile_pool(name="work", bufs=3))
-        small = ctx.enter_context(tc.tile_pool(name="small", bufs=4))
+        work = ctx.enter_context(tc.tile_pool(name="work", bufs=4))
+        small = ctx.enter_context(tc.tile_pool(name="small", bufs=5))
         batch = ctx.enter_context(tc.tile_pool(name="batch", bufs=3))
         ps_s = ctx.enter_context(tc.psum_pool(name="ps_s", bufs=2 * G))
         ps_e = ctx.enter_context(tc.psum_pool(name="ps_e", bufs=2))
@@ -69,52 +69,61 @@ def tile_scaleddotproductattention_kernel(tc, Q, K, V, mask, out):
         live = {}
 
 
-        def load_head(h):
-            k_sb = raw.tile([P, G, PACK, D], BF16, tag="k_sb")
-            nc.sync.dma_start(out=k_sb[:], in_=K[0, h].rearrange("(g p t) d -> p g t d", g=G, t=PACK))
+        def load_k_and_q(h):
+            k_sb = raw.tile([P, WB, PAIR, D], BF16, tag="k_sb")
+            k_rows = K[0, h].rearrange("(x r u e) d -> u e r x d", x=WB, u=PAIR, e=PAIR)
+            for u in range(PAIR):
+                for e in range(PAIR):
+                    nc.sync.dma_start(out=k_sb[e::PAIR, :, u, :], in_=k_rows[u, e])
             q_sb = raw.tile([P, NJ, D], BF16, tag="q_sb")
             nc.sync.dma_start(out=q_sb[:], in_=Q[0, h].rearrange("(p j) d -> p j d", j=NJ))
-            v_sb = raw.tile([P, G, PACK, D], BF16, tag="v_sb")
-            nc.sync.dma_start(out=v_sb[:], in_=V[0, h].rearrange("(g p t) d -> p g t d", g=G, t=PACK))
             live["k_sb", h] = k_sb
             live["q_sb", h] = q_sb
+
+        def load_v(h):
+            v_sb = raw.tile([P, G, PACK, D], BF16, tag="v_sb")
+            nc.sync.dma_start(out=v_sb[:], in_=V[0, h].rearrange("(g p t) d -> p g t d", g=G, t=PACK))
             live["v_sb", h] = v_sb
 
         def transpose_k_and_q(h):
             pk = ps_t.tile([P, PLANES, P], BF16, tag="tr")
             for g in range(G):
-                for t in range(PACK):
-                    nc.tensor.transpose(
-                        out=pk[:, g * PACK + t, :], in_=live["k_sb", h][:, g, t, :], identity=ident_bf[:]
-                    )
+                for u in range(PAIR):
+                    for b in range(PAIR):
+                        nc.tensor.transpose(
+                            out=pk[:, (g * PAIR + u) * PAIR + b, :],
+                            in_=live["k_sb", h][:, g * PAIR + b, u, :],
+                            identity=ident_bf[:],
+                        )
             pq = ps_o.tile([P, NJ, P], BF16, tag="o")
             for j in range(NJ):
                 nc.tensor.transpose(out=pq[:, j, :], in_=live["q_sb", h][:, j, :], identity=ident_bf[:])
             live["pk", h] = pk
             live["pq", h] = pq
 
-        def copy_k_and_q(h):
+        def copy_k(h):
             k_t = heads.tile([P, N], BF16, tag="k_t")
-            nc.vector.tensor_copy(
-                out=k_t[:].rearrange("d (a p e) -> d a p e", a=WB, e=PAIR),
-                in_=live["pk", h][:].rearrange("d (a e) p -> d a p e", e=PAIR),
-            )
+            nc.vector.tensor_copy(out=k_t[:], in_=live["pk", h][:].rearrange("d c p -> d (c p)"))
+            live["k_t", h] = k_t
+
+        def copy_q(h):
             q_t = heads.tile([P, NJ, P], BF16, tag="q_t")
             nc.scalar.copy(out=q_t[:], in_=live["pq", h][:])
-            live["k_t", h] = k_t
             live["q_t", h] = q_t
 
-        def group_v(h):
-            v_g = heads.tile([P, G, D, PACK], BF16, tag="v_g", align_bytes=64)
+        def group_v(h, piece):
+            if piece == 0:
+                live["v_g", h] = heads.tile([P, G, D, PACK], BF16, tag="v_g", align_bytes=64, name="v_g")
+            g, half = divmod(piece, 2)
+            cols = slice(half * D // 2, (half + 1) * D // 2)
             nc.gpsimd.tensor_scalar(
-                out=v_g[:],
-                in0=live["v_sb", h][:].rearrange("p g t d -> p g d t"),
+                out=live["v_g", h][:, g, cols, :],
+                in0=live["v_sb", h][:, g, :, cols].rearrange("p t d -> p d t"),
                 scalar1=1.0,
                 scalar2=0.0,
                 op0=ALU.mult,
                 op1=ALU.add,
             )
-            live["v_g", h] = v_g
 
         def quantise_v(h):
             v_codes = heads.tile([P, G * D], U32, tag="v_codes", align_bytes=64)
@@ -130,20 +139,24 @@ def tile_scaleddotproductattention_kernel(tc, Q, K, V, mask, out):
 
         def load_mask(j):
             mi = mstage.tile([P, 2 * N], I32, tag="mi", bufs=NJ)
-            nc.sync.dma_start(out=mi[:], in_=mask_words[:, j, :])
+            for g in range(G):
+                nc.sync.dma_start(out=mi[:, g * N : (g + 1) * N], in_=mask_words[:, j, g * N : (g + 1) * N])
             live["mi", j] = mi
 
         def convert_mask(j):
             mf = mstage.tile([P, G, PACK, P], F32, tag="mf")
-            words = live["mi", j][:].rearrange("q (g p u e w) -> q g u p e w", g=G, p=P, u=PAIR, e=PAIR, w=2)
+            words = live["mi", j][:].rearrange(
+                "q (g b r u e w) -> q g u b r e w", g=G, b=PAIR, r=P // PAIR, u=PAIR, e=PAIR, w=2
+            )
             for g in range(G):
-                nc.vector.tensor_scalar(
-                    out=mf[:, g].rearrange("q r c -> q (r c)").rearrange("q (u p e) -> q u p e", u=PAIR, e=PAIR),
-                    in0=words[:, g, :, :, :, 0],
-                    scalar1=MASKED,
-                    scalar2=None,
-                    op0=ALU.mult,
-                )
+                for u in range(PAIR):
+                    nc.vector.tensor_scalar(
+                        out=mf[:, g, u * PAIR : (u + 1) * PAIR, :].rearrange("q b (r e) -> q b r e", e=PAIR),
+                        in0=words[:, g, u, :, :, :, 0],
+                        scalar1=MASKED,
+                        scalar2=None,
+                        op0=ALU.mult,
+                    )
             live["mf", j] = mf
 
         def transpose_mask(j):
@@ -184,21 +197,19 @@ def tile_scaleddotproductattention_kernel(tc, Q, K, V, mask, out):
                 stop=True,
             )
 
-        def row_max(i):
-            neg_s = work.tile([P, G, BANK], F32, tag="neg_s")
-            neg_m2 = small.tile([P, G], F32, tag="neg_m2")
-            for g in range(G):
-                nc.vector.tensor_scalar(
-                    out=neg_s[:, g, :],
-                    in0=live["sp", i, g][:],
-                    scalar1=-SCALE,
-                    scalar2=None,
-                    op0=ALU.mult,
-                    op1=ALU.min,
-                    accum_out=neg_m2[:, g : g + 1],
-                )
-            live["neg_s", i] = neg_s
-            live["neg_m2", i] = neg_m2
+        def row_max(i, g):
+            if g == 0:
+                live["neg_s", i] = work.tile([P, G, BANK], F32, tag="neg_s", name="neg_s")
+                live["neg_m2", i] = small.tile([P, G], F32, tag="neg_m2", name="neg_m2")
+            nc.vector.tensor_scalar(
+                out=live["neg_s", i][:, g, :],
+                in0=live["sp", i, g][:],
+                scalar1=-SCALE,
+                scalar2=None,
+                op0=ALU.mult,
+                op1=ALU.min,
+                accum_out=live["neg_m2", i][:, g : g + 1],
+            )
 
         def join_row_max(i):
             neg_m = small.tile([P, 1], F32, tag="neg_m")
@@ -235,7 +246,7 @@ def tile_scaleddotproductattention_kernel(tc, Q, K, V, mask, out):
                 nc.tensor.transpose(out=live["et", i][:, a, :], in_=e_words[:, a * P : (a + 1) * P], identity=ident_f[:])
 
         def copy_e(i):
-            grouped = batch.tile([P, G, P, PACK], BF16, tag="grouped", align_bytes=64)
+            grouped = batch.tile([P, G, P, PACK], BF16, tag="grouped", align_bytes=64, bufs=4)
             nc.scalar.copy(
                 out=grouped[:]
                 .rearrange("p g q t -> p (g q t)")
@@ -315,14 +326,19 @@ def tile_scaleddotproductattention_kernel(tc, Q, K, V, mask, out):
                 stage(index, *more)
 
 
-        load_head(0)
-        for j in range(NJ):
+        load_k_and_q(0)
+        load_mask(0)
+        load_mask(1)
+        load_v(0)
+        for j in range(2, NJ):
             load_mask(j)
-        load_head(1)
+        load_k_and_q(1)
+        load_v(1)
 
         for k in range(-3, LAST_STEP + 1):
-            run(load_head, head_at(k, 13))
-            run(copy_k_and_q, head_to_transpose(k - 1))
+            run(load_k_and_q, head_at(k, 13))
+            run(load_v, head_at(k, 13))
+            run(copy_q, head_to_transpose(k - 1))
             run(transpose_mask, mask_tile_at(k, 1))
             run(copy_mask, mask_tile_at(k, 1))
             run(mask_scores, unit_at(k, 0), 0)
@@ -333,12 +349,15 @@ def tile_scaleddotproductattention_kernel(tc, Q, K, V, mask, out):
             run(transpose_e, unit_at(k, LAG_TRANSPOSE), range(WB))
             run(transpose_k_and_q, head_to_transpose(k))
             run(convert_mask, mask_tile_at(k, 2))
-            run(row_max, unit_at(k, LAG_MAX))
+            run(row_max, unit_at(k, LAG_MAX), 0)
+            run(quantise_e, unit_at(k, LAG_QUANTISE))
+            run(quantise_v, head_at(k, -5))
+            run(row_max, unit_at(k, LAG_MAX), 1)
             run(join_row_max, unit_at(k, LAG_MAX))
+            run(copy_k, head_to_transpose(k - 1))
+            for piece in range(PACK):
+                run(group_v, head_at(k, -1 - piece), piece)
             run(exponent, unit_at(k, LAG_EXP))
             run(copy_e, unit_at(k, LAG_COPY))
-            run(group_v, head_at(k, -4))
-            run(quantise_e, unit_at(k, LAG_QUANTISE))
             run(divide_and_store, batch_at(k, LAG_DIVIDE))
             run(reciprocals, batch_at(k, LAG_RECIPROCAL))
-            run(quantise_v, head_at(k, -5))

@@ -40,7 +40,7 @@ LAG_RECIPROCAL = 4
 LAG_PV = 8
 LAG_DIVIDE = 9
 LAST_STEP = UNITS - 1 + LAG_DIVIDE
-CODE_BUFS = UB - 1 + LAG_PV - LAG_QUANTISE + 2
+CODE_BUFS = 4
 
 
 def tile_scaleddotproductattention_kernel(tc, Q, K, V, mask, out):
@@ -53,10 +53,7 @@ def tile_scaleddotproductattention_kernel(tc, Q, K, V, mask, out):
         work = ctx.enter_context(tc.tile_pool(name="work", bufs=4))
         small = ctx.enter_context(tc.tile_pool(name="small", bufs=5))
         batch = ctx.enter_context(tc.tile_pool(name="batch", bufs=3))
-        ps_s = ctx.enter_context(tc.psum_pool(name="ps_s", bufs=2 * G))
-        ps_e = ctx.enter_context(tc.psum_pool(name="ps_e", bufs=2))
-        ps_o = ctx.enter_context(tc.psum_pool(name="ps_o", bufs=1))
-        ps_t = ctx.enter_context(tc.psum_pool(name="ps_t", bufs=1))
+        psum = ctx.enter_context(tc.psum_pool(name="psum", bufs=8))
         ctx.enter_context(tc.manual_schedule())
 
         ident_bf = const.tile([P, P], BF16)
@@ -85,8 +82,8 @@ def tile_scaleddotproductattention_kernel(tc, Q, K, V, mask, out):
             nc.sync.dma_start(out=v_sb[:], in_=V[0, h].rearrange("(g p t) d -> p g t d", g=G, t=PACK))
             live["v_sb", h] = v_sb
 
-        def transpose_k_and_q(h):
-            pk = ps_t.tile([P, PLANES, P], BF16, tag="tr")
+        def transpose_k(h):
+            pk = psum.tile([P, PLANES, P], BF16, tag="bank")
             for g in range(G):
                 for u in range(PAIR):
                     for b in range(PAIR):
@@ -95,10 +92,12 @@ def tile_scaleddotproductattention_kernel(tc, Q, K, V, mask, out):
                             in_=live["k_sb", h][:, g * PAIR + b, u, :],
                             identity=ident_bf[:],
                         )
-            pq = ps_o.tile([P, NJ, P], BF16, tag="o")
+            live["pk", h] = pk
+
+        def transpose_q(h):
+            pq = psum.tile([P, NJ, P], BF16, tag="bank")
             for j in range(NJ):
                 nc.tensor.transpose(out=pq[:, j, :], in_=live["q_sb", h][:, j, :], identity=ident_bf[:])
-            live["pk", h] = pk
             live["pq", h] = pq
 
         def copy_k(h):
@@ -160,9 +159,8 @@ def tile_scaleddotproductattention_kernel(tc, Q, K, V, mask, out):
             live["mf", j] = mf
 
         def transpose_mask(j):
-            live["pm", j, 0] = ps_t.tile([P, PACK, P], F32, tag="tr", name="pm0")
-            live["pm", j, 1] = ps_o.tile([P, PACK, P], F32, tag="o", name="pm1")
             for g in range(G):
+                live["pm", j, g] = psum.tile([P, PACK, P], F32, tag="bank", name="pm")
                 for t in range(PACK):
                     nc.tensor.transpose(
                         out=live["pm", j, g][:, t, :], in_=live["mf", j][:, g, t, :], identity=ident_f[:]
@@ -175,7 +173,7 @@ def tile_scaleddotproductattention_kernel(tc, Q, K, V, mask, out):
 
         def mask_scores(i, g):
             h, j = divmod(i, NJ)
-            sp = ps_s.tile([P, BANK], F32, tag="s")
+            sp = psum.tile([P, BANK], F32, tag="bank")
             for t in range(PACK):
                 nc.tensor.matmul(
                     out=sp[:, t * P : (t + 1) * P],
@@ -240,32 +238,38 @@ def tile_scaleddotproductattention_kernel(tc, Q, K, V, mask, out):
 
         def transpose_e(i, blocks):
             if ("et", i) not in live:
-                live["et", i] = ps_e.tile([P, WB, P], F32, tag="et", name="et")
+                live["et", i] = psum.tile([P, WB, P], F32, tag="bank", name="et")
             e_words = live["e", i][:].bitcast(F32)
             for a in blocks:
                 nc.tensor.transpose(out=live["et", i][:, a, :], in_=e_words[:, a * P : (a + 1) * P], identity=ident_f[:])
 
         def copy_e(i):
-            grouped = batch.tile([P, G, P, PACK], BF16, tag="grouped", align_bytes=64, bufs=4)
+            pair, half = divmod(i, 2)
+            if half == 0:
+                live["grouped", pair] = batch.tile(
+                    [P, 2, G, P, PACK], BF16, tag="grouped", align_bytes=64, bufs=3, name="grouped"
+                )
             nc.scalar.copy(
-                out=grouped[:]
+                out=live["grouped", pair][:, half]
                 .rearrange("p g q t -> p (g q t)")
                 .bitcast(F32)
                 .rearrange("p (g q u) -> p g q u", g=G, u=PAIR),
                 in_=live["et", i][:].rearrange("p (g u) q -> p g q u", u=PAIR),
             )
-            live["grouped", i] = grouped
 
         def quantise_e(i):
-            codes = batch.tile([P, G, P], U32, tag="codes", align_bytes=64, bufs=CODE_BUFS)
-            scales = batch.tile([P, G, P], U8, tag="scales", align_bytes=64, bufs=CODE_BUFS)
+            pair, half = divmod(i, 2)
+            if half == 0:
+                return
+            codes = batch.tile([P, 2, G, P], U32, tag="codes", align_bytes=64, bufs=CODE_BUFS)
+            scales = batch.tile([P, 2, G, P], U8, tag="scales", align_bytes=64, bufs=CODE_BUFS)
             nc.vector.quantize_mx(
-                out=codes[:].rearrange("p g q -> p (g q)").bitcast(FP8X4),
-                scales=scales[:].rearrange("p g q -> p (g q)"),
-                in_=live["grouped", i][:].rearrange("p g q t -> p (g q t)"),
+                out=codes[:].rearrange("p i g q -> p (i g q)").bitcast(FP8X4),
+                scales=scales[:].rearrange("p i g q -> p (i g q)"),
+                in_=live["grouped", pair][:].rearrange("p i g q t -> p (i g q t)"),
             )
-            live["codes", i] = codes
-            live["scales", i] = scales
+            live["codes", pair] = codes
+            live["scales", pair] = scales
 
 
         def reciprocals(b):
@@ -275,13 +279,14 @@ def tile_scaleddotproductattention_kernel(tc, Q, K, V, mask, out):
 
         def e_times_v(b):
             h = b * UB // NJ
-            o_ps = ps_o.tile([P, UB, D], F32, tag="o")
+            o_ps = psum.tile([P, UB, D], F32, tag="bank")
             for u in range(UB):
+                pair, half = divmod(b * UB + u, 2)
                 for g in range(G):
                     nc.tensor.matmul_mx(
                         out=o_ps[:, u, :],
-                        lhsT=live["codes", b * UB + u][:, g, :].bitcast(FP8X4),
-                        lhsT_scale=live["scales", b * UB + u][:, g, :],
+                        lhsT=live["codes", pair][:, half, g, :].bitcast(FP8X4),
+                        lhsT_scale=live["scales", pair][:, half, g, :],
                         rhs=live["v_codes", h][:, g * D : (g + 1) * D].bitcast(FP8X4),
                         rhs_scale=live["v_scales", h][:, g * D : (g + 1) * D],
                         start=(g == 0),
@@ -315,12 +320,6 @@ def tile_scaleddotproductattention_kernel(tc, Q, K, V, mask, out):
         def mask_tile_at(k, lead):
             return k + lead if 0 <= k + lead < NJ else None
 
-        def head_to_transpose(k):
-            if k == NJ - 2:
-                return 1
-            h = head_at(k, 3)
-            return None if h == 1 else h
-
         def run(stage, index, *more):
             if index is not None:
                 stage(index, *more)
@@ -338,26 +337,27 @@ def tile_scaleddotproductattention_kernel(tc, Q, K, V, mask, out):
         for k in range(-3, LAST_STEP + 1):
             run(load_k_and_q, head_at(k, 13))
             run(load_v, head_at(k, 13))
-            run(copy_q, head_to_transpose(k - 1))
-            run(transpose_mask, mask_tile_at(k, 1))
-            run(copy_mask, mask_tile_at(k, 1))
-            run(mask_scores, unit_at(k, 0), 0)
-            run(mask_scores, unit_at(k, 0), 1)
-            run(q_times_k, unit_at(k, 0), 0)
-            run(e_times_v, batch_at(k, LAG_PV))
-            run(q_times_k, unit_at(k, 0), 1)
-            run(transpose_e, unit_at(k, LAG_TRANSPOSE), range(WB))
-            run(transpose_k_and_q, head_to_transpose(k))
+            run(copy_mask, mask_tile_at(k, 0))
             run(convert_mask, mask_tile_at(k, 2))
             run(row_max, unit_at(k, LAG_MAX), 0)
             run(quantise_e, unit_at(k, LAG_QUANTISE))
             run(quantise_v, head_at(k, -5))
             run(row_max, unit_at(k, LAG_MAX), 1)
             run(join_row_max, unit_at(k, LAG_MAX))
-            run(copy_k, head_to_transpose(k - 1))
+            run(copy_k, head_at(k, 2))
             for piece in range(PACK):
                 run(group_v, head_at(k, -1 - piece), piece)
             run(exponent, unit_at(k, LAG_EXP))
+            run(copy_q, head_at(k, 1))
             run(copy_e, unit_at(k, LAG_COPY))
             run(divide_and_store, batch_at(k, LAG_DIVIDE))
             run(reciprocals, batch_at(k, LAG_RECIPROCAL))
+            run(mask_scores, unit_at(k, 0), 0)
+            run(mask_scores, unit_at(k, 0), 1)
+            run(q_times_k, unit_at(k, 0), 0)
+            run(e_times_v, batch_at(k, LAG_PV))
+            run(q_times_k, unit_at(k, 0), 1)
+            run(transpose_e, unit_at(k, LAG_TRANSPOSE), range(WB))
+            run(transpose_mask, mask_tile_at(k, 1))
+            run(transpose_k, head_at(k, 3))
+            run(transpose_q, head_at(k, 2))

@@ -28,7 +28,9 @@ UB = 4
 UNITS = H * NJ
 BATCHES = UNITS // UB
 SCALE = 1.0 / math.sqrt(D)
-MASKED = -1.0e12 * math.sqrt(D)
+MASKED = -(2.0**43)
+PAIRED = 2 * NJ
+MATMUL_MASKED = 12
 FLOPS = 4 * H * N * N * D
 
 LAG_MAX = 1
@@ -62,6 +64,9 @@ def tile_scaleddotproductattention_kernel(tc, Q, K, V, mask, out):
         make_identity(nc, ident_f[:])
         mask_t = const.tile([P, PLANES, NJ, P], F32)
         mask_words = mask.bitcast(I32).rearrange("(p j) w -> p j w", j=NJ)
+
+        def head_and_tile(i):
+            return (i % 2, i // 2) if i < PAIRED else divmod(i, NJ)
 
         live = {}
 
@@ -143,7 +148,7 @@ def tile_scaleddotproductattention_kernel(tc, Q, K, V, mask, out):
             live["mi", j] = mi
 
         def convert_mask(j):
-            mf = mstage.tile([P, G, PACK, P], F32, tag="mf")
+            mf = mstage.tile([P, G, PACK, P], BF16, tag="mf", bufs=NJ)
             words = live["mi", j][:].rearrange(
                 "q (g b r u e w) -> q g u b r e w", g=G, b=PAIR, r=P // PAIR, u=PAIR, e=PAIR, w=2
             )
@@ -159,21 +164,30 @@ def tile_scaleddotproductattention_kernel(tc, Q, K, V, mask, out):
             live["mf", j] = mf
 
         def transpose_mask(j):
-            for g in range(G):
-                live["pm", j, g] = psum.tile([P, PACK, P], F32, tag="bank", name="pm")
-                for t in range(PACK):
-                    nc.tensor.transpose(
-                        out=live["pm", j, g][:, t, :], in_=live["mf", j][:, g, t, :], identity=ident_f[:]
-                    )
+            pm = psum.tile([P, PLANES, P], BF16, tag="bank")
+            for c in range(PLANES):
+                nc.tensor.transpose(
+                    out=pm[:, c, :], in_=live["mf", j][:, c // PACK, c % PACK, :], identity=ident_bf[:]
+                )
+            live["pm", j] = pm
 
         def copy_mask(j):
-            for g in range(G):
-                nc.scalar.copy(out=mask_t[:, g * PACK : (g + 1) * PACK, j, :], in_=live["pm", j, g][:])
+            nc.scalar.copy(out=mask_t[:, :, j, :], in_=live["pm", j][:])
 
 
         def mask_scores(i, g):
-            h, j = divmod(i, NJ)
+            h, j = head_and_tile(i)
             sp = psum.tile([P, BANK], F32, tag="bank")
+            live["sp", i, g] = sp
+            if i < MATMUL_MASKED:
+                nc.tensor.matmul(
+                    out=sp[:],
+                    lhsT=ident_bf[:],
+                    rhs=live["mf", j][:, g].rearrange("q t p -> q (t p)"),
+                    start=True,
+                    stop=False,
+                )
+                return
             for t in range(PACK):
                 nc.tensor.matmul(
                     out=sp[:, t * P : (t + 1) * P],
@@ -183,10 +197,9 @@ def tile_scaleddotproductattention_kernel(tc, Q, K, V, mask, out):
                     start=(t == 0),
                     stop=False,
                 )
-            live["sp", i, g] = sp
 
         def q_times_k(i, g):
-            h, j = divmod(i, NJ)
+            h, j = head_and_tile(i)
             nc.tensor.matmul(
                 out=live["sp", i, g][:],
                 lhsT=live["q_t", h][:, j, :],
@@ -278,9 +291,9 @@ def tile_scaleddotproductattention_kernel(tc, Q, K, V, mask, out):
             live["rinv", b] = rinv
 
         def e_times_v(b):
-            h = b * UB // NJ
             o_ps = psum.tile([P, UB, D], F32, tag="bank")
             for u in range(UB):
+                h, j = head_and_tile(b * UB + u)
                 pair, half = divmod(b * UB + u, 2)
                 for g in range(G):
                     nc.tensor.matmul_mx(
@@ -295,7 +308,6 @@ def tile_scaleddotproductattention_kernel(tc, Q, K, V, mask, out):
             live["o_ps", b] = o_ps
 
         def divide_and_store(b):
-            h, j0 = divmod(b * UB, NJ)
             o_sb = batch.tile([P, UB, D], F32, tag="o_sb")
             nc.vector.tensor_tensor(
                 out=o_sb[:],
@@ -303,7 +315,14 @@ def tile_scaleddotproductattention_kernel(tc, Q, K, V, mask, out):
                 in1=live["rinv", b][:].unsqueeze(2).to_broadcast([P, UB, D]),
                 op=ALU.mult,
             )
-            nc.sync.dma_start(out=out[0, h].rearrange("(p j) d -> p j d", j=NJ)[:, j0 : j0 + UB, :], in_=o_sb[:])
+            h, j0 = head_and_tile(b * UB)
+            if b * UB < PAIRED:
+                for h in range(2):
+                    rows = out[0, h].rearrange("(p j) d -> p j d", j=NJ)
+                    nc.sync.dma_start(out=rows[:, j0 : j0 + 2, :], in_=o_sb[:, h::2, :])
+            else:
+                rows = out[0, h].rearrange("(p j) d -> p j d", j=NJ)
+                nc.sync.dma_start(out=rows[:, j0 : j0 + UB, :], in_=o_sb[:])
 
 
         def unit_at(k, lag):
@@ -313,12 +332,27 @@ def tile_scaleddotproductattention_kernel(tc, Q, K, V, mask, out):
             b, u = divmod(k - lag, UB)
             return b if u == UB - 1 and 0 <= b < BATCHES else None
 
-        def head_at(k, lead):
-            h, j = divmod(k + lead, NJ)
-            return h if j == 0 and 0 <= h < H else None
+        def first_unit(h):
+            return h if h < 2 else h * NJ
 
-        def mask_tile_at(k, lead):
-            return k + lead if 0 <= k + lead < NJ else None
+        def head_at(k, lag):
+            return next_of(H, lambda h: first_unit(h) + lag == k)
+
+        def next_of(count, test):
+            found = [n for n in range(count) if test(n)]
+            return found[0] if found else None
+
+        def head_with_k(k):
+            return next_of(H, lambda h: first_unit(h) - (1 if h < 2 else 3) == k)
+
+        def head_with_q(k):
+            return next_of(H, lambda h: first_unit(h) - (1 if h < 2 else 2) == k)
+
+        def mask_tile_to_convert(k):
+            return next_of(NJ, lambda j: max(0, min(2 * j - 1, j + 3)) == k)
+
+        def mask_tile_at(k, lag):
+            return k - lag if 0 <= k - lag < NJ else None
 
         def run(stage, index, *more):
             if index is not None:
@@ -327,29 +361,33 @@ def tile_scaleddotproductattention_kernel(tc, Q, K, V, mask, out):
 
         load_k_and_q(0)
         load_mask(0)
+        load_k_and_q(1)
         load_mask(1)
         load_v(0)
+        load_v(1)
         for j in range(2, NJ):
             load_mask(j)
-        load_k_and_q(1)
-        load_v(1)
 
-        for k in range(-3, LAST_STEP + 1):
-            run(load_k_and_q, head_at(k, 13))
-            run(load_v, head_at(k, 13))
-            run(copy_mask, mask_tile_at(k, 0))
-            run(convert_mask, mask_tile_at(k, 2))
+        for k in range(-1, LAST_STEP + 1):
+            h = head_at(k, -13)
+            if h is not None and h > 1:
+                load_k_and_q(h)
+                load_v(h)
             run(row_max, unit_at(k, LAG_MAX), 0)
             run(quantise_e, unit_at(k, LAG_QUANTISE))
-            run(quantise_v, head_at(k, -5))
+            run(quantise_v, head_at(k, 6))
             run(row_max, unit_at(k, LAG_MAX), 1)
             run(join_row_max, unit_at(k, LAG_MAX))
-            run(copy_k, head_at(k, 2))
-            for piece in range(PACK):
-                run(group_v, head_at(k, -1 - piece), piece)
+            run(copy_k, head_with_k(k - 1))
+            run(convert_mask, mask_tile_to_convert(k))
+            for h in range(H):
+                piece = k - first_unit(h) - 2
+                if 0 <= piece < PACK:
+                    group_v(h, piece)
             run(exponent, unit_at(k, LAG_EXP))
-            run(copy_q, head_at(k, 1))
+            run(copy_q, head_with_q(k - 1))
             run(copy_e, unit_at(k, LAG_COPY))
+            run(copy_mask, mask_tile_at(k, 4))
             run(divide_and_store, batch_at(k, LAG_DIVIDE))
             run(reciprocals, batch_at(k, LAG_RECIPROCAL))
             run(mask_scores, unit_at(k, 0), 0)
@@ -358,6 +396,6 @@ def tile_scaleddotproductattention_kernel(tc, Q, K, V, mask, out):
             run(e_times_v, batch_at(k, LAG_PV))
             run(q_times_k, unit_at(k, 0), 1)
             run(transpose_e, unit_at(k, LAG_TRANSPOSE), range(WB))
-            run(transpose_mask, mask_tile_at(k, 1))
-            run(transpose_k, head_at(k, 3))
-            run(transpose_q, head_at(k, 2))
+            run(transpose_mask, mask_tile_at(k, 3))
+            run(transpose_k, head_with_k(k))
+            run(transpose_q, head_with_q(k))

@@ -42,7 +42,6 @@ LAG_RECIPROCAL = 4
 LAG_PV = 8
 LAG_DIVIDE = 9
 LAST_STEP = UNITS - 1 + LAG_DIVIDE
-CODE_BUFS = 4
 
 
 def tile_scaleddotproductattention_kernel(tc, Q, K, V, mask, out):
@@ -105,9 +104,16 @@ def tile_scaleddotproductattention_kernel(tc, Q, K, V, mask, out):
                 nc.tensor.transpose(out=pq[:, j, :], in_=live["q_sb", h][:, j, :], identity=ident_bf[:])
             live["pq", h] = pq
 
+        def on_scalar(h):
+            return h % 2 == 1
+
         def copy_k(h):
             k_t = heads.tile([P, N], BF16, tag="k_t")
-            nc.vector.tensor_copy(out=k_t[:], in_=live["pk", h][:].rearrange("d c p -> d (c p)"))
+            k_ps = live["pk", h][:].rearrange("d c p -> d (c p)")
+            if on_scalar(h):
+                nc.scalar.copy(out=k_t[:], in_=k_ps)
+            else:
+                nc.vector.tensor_copy(out=k_t[:], in_=k_ps)
             live["k_t", h] = k_t
 
         def copy_q(h):
@@ -236,8 +242,8 @@ def tile_scaleddotproductattention_kernel(tc, Q, K, V, mask, out):
 
         def exponent(i):
             b, u = divmod(i, UB)
-            if u == 0:
-                live["rowsum", b] = batch.tile([P, UB], F32, tag="rowsum", name="rowsum", bufs=4)
+            if i % (2 * UB) == 0:
+                live["rowsum", b // 2] = batch.tile([P, 2, UB], F32, tag="rowsum", name="rowsum")
             e = work.tile([P, N], BF16, tag="e")
             nc.scalar.activation(
                 out=e[:],
@@ -245,7 +251,7 @@ def tile_scaleddotproductattention_kernel(tc, Q, K, V, mask, out):
                 func=ACTF.Exp,
                 bias=live["neg_m", i][:, 0:1],
                 scale=-1.0,
-                accum_out=live["rowsum", b][:, u : u + 1],
+                accum_out=live["rowsum", b // 2][:, b % 2, u : u + 1],
             )
             live["e", i] = e
 
@@ -257,49 +263,46 @@ def tile_scaleddotproductattention_kernel(tc, Q, K, V, mask, out):
                 nc.tensor.transpose(out=live["et", i][:, a, :], in_=e_words[:, a * P : (a + 1) * P], identity=ident_f[:])
 
         def copy_e(i):
-            pair, half = divmod(i, 2)
-            if half == 0:
-                live["grouped", pair] = batch.tile(
-                    [P, 2, G, P, PACK], BF16, tag="grouped", align_bytes=64, bufs=3, name="grouped"
+            b, u = divmod(i, UB)
+            if u == 0:
+                live["grouped", b] = batch.tile(
+                    [P, UB, G, P, PACK], BF16, tag="grouped", align_bytes=64, bufs=3, name="grouped"
                 )
             nc.scalar.copy(
-                out=live["grouped", pair][:, half]
+                out=live["grouped", b][:, u]
                 .rearrange("p g q t -> p (g q t)")
                 .bitcast(F32)
                 .rearrange("p (g q u) -> p g q u", g=G, u=PAIR),
                 in_=live["et", i][:].rearrange("p (g u) q -> p g q u", u=PAIR),
             )
 
-        def quantise_e(i):
-            pair, half = divmod(i, 2)
-            if half == 0:
-                return
-            codes = batch.tile([P, 2, G, P], U32, tag="codes", align_bytes=64, bufs=CODE_BUFS)
-            scales = batch.tile([P, 2, G, P], U8, tag="scales", align_bytes=64, bufs=CODE_BUFS)
+
+        def quantise_e(b):
+            codes = batch.tile([P, UB, G, P], U32, tag="codes", align_bytes=64, bufs=2)
+            scales = batch.tile([P, UB, G, P], U8, tag="scales", align_bytes=64, bufs=2)
             nc.vector.quantize_mx(
                 out=codes[:].rearrange("p i g q -> p (i g q)").bitcast(FP8X4),
                 scales=scales[:].rearrange("p i g q -> p (i g q)"),
-                in_=live["grouped", pair][:].rearrange("p i g q t -> p (i g q t)"),
+                in_=live["grouped", b][:].rearrange("p i g q t -> p (i g q t)"),
             )
-            live["codes", pair] = codes
-            live["scales", pair] = scales
-
+            live["codes", b] = codes
+            live["scales", b] = scales
 
         def reciprocals(b):
-            rinv = batch.tile([P, UB], F32, tag="rinv")
-            nc.vector.reciprocal(out=rinv[:], in_=live["rowsum", b][:])
-            live["rinv", b] = rinv
+            if b % 2 == 1:
+                rinv = batch.tile([P, 2, UB], F32, tag="rinv")
+                nc.vector.reciprocal(out=rinv[:], in_=live["rowsum", b // 2][:])
+                live["rinv", b // 2] = rinv
 
         def e_times_v(b):
             o_ps = psum.tile([P, UB, D], F32, tag="bank")
             for u in range(UB):
                 h, j = head_and_tile(b * UB + u)
-                pair, half = divmod(b * UB + u, 2)
                 for g in range(G):
                     nc.tensor.matmul_mx(
                         out=o_ps[:, u, :],
-                        lhsT=live["codes", pair][:, half, g, :].bitcast(FP8X4),
-                        lhsT_scale=live["scales", pair][:, half, g, :],
+                        lhsT=live["codes", b][:, u, g, :].bitcast(FP8X4),
+                        lhsT_scale=live["scales", b][:, u, g, :],
                         rhs=live["v_codes", h][:, g * D : (g + 1) * D].bitcast(FP8X4),
                         rhs_scale=live["v_scales", h][:, g * D : (g + 1) * D],
                         start=(g == 0),
@@ -312,7 +315,7 @@ def tile_scaleddotproductattention_kernel(tc, Q, K, V, mask, out):
             nc.vector.tensor_tensor(
                 out=o_sb[:],
                 in0=live["o_ps", b][:],
-                in1=live["rinv", b][:].unsqueeze(2).to_broadcast([P, UB, D]),
+                in1=live["rinv", b // 2][:, b % 2, :].unsqueeze(2).to_broadcast([P, UB, D]),
                 op=ALU.mult,
             )
             h, j0 = head_and_tile(b * UB)
@@ -374,17 +377,21 @@ def tile_scaleddotproductattention_kernel(tc, Q, K, V, mask, out):
                 load_k_and_q(h)
                 load_v(h)
             run(row_max, unit_at(k, LAG_MAX), 0)
-            run(quantise_e, unit_at(k, LAG_QUANTISE))
+            run(quantise_e, batch_at(k, LAG_QUANTISE))
             run(quantise_v, head_at(k, 6))
             run(row_max, unit_at(k, LAG_MAX), 1)
             run(join_row_max, unit_at(k, LAG_MAX))
-            run(copy_k, head_with_k(k - 1))
+            k_head = head_with_k(k - 1)
+            if k_head is not None and not on_scalar(k_head):
+                copy_k(k_head)
             run(convert_mask, mask_tile_to_convert(k))
             for h in range(H):
                 piece = k - first_unit(h) - 2
                 if 0 <= piece < PACK:
                     group_v(h, piece)
             run(exponent, unit_at(k, LAG_EXP))
+            if k_head is not None and on_scalar(k_head):
+                copy_k(k_head)
             run(copy_q, head_with_q(k - 1))
             run(copy_e, unit_at(k, LAG_COPY))
             run(copy_mask, mask_tile_at(k, 4))

@@ -30,7 +30,7 @@ BATCHES = UNITS // UB
 SCALE = 1.0 / math.sqrt(D)
 MASKED = -(2.0**43)
 PAIRED = 2 * NJ
-MATMUL_MASKED = 12
+EARLY = 3
 FLOPS = 4 * H * N * N * D
 
 LAG_MAX = 1
@@ -63,6 +63,7 @@ def tile_scaleddotproductattention_kernel(tc, Q, K, V, mask, out):
         make_identity(nc, ident_f[:])
         mask_t = const.tile([P, PLANES, NJ, P], F32)
         mask_words = mask.bitcast(I32).rearrange("(p j) w -> p j w", j=NJ)
+        mask_bytes = mask.bitcast(U8).rearrange("q b -> (q b)")[8 * N - 1 : 8 * N * N - 1].rearrange("(r b) -> r b", b=8 * N)
 
         def head_and_tile(i):
             return (i % 2, i // 2) if i < PAIRED else divmod(i, NJ)
@@ -71,11 +72,8 @@ def tile_scaleddotproductattention_kernel(tc, Q, K, V, mask, out):
 
 
         def load_k_and_q(h):
-            k_sb = raw.tile([P, WB, PAIR, D], BF16, tag="k_sb")
-            k_rows = K[0, h].rearrange("(x r u e) d -> u e r x d", x=WB, u=PAIR, e=PAIR)
-            for u in range(PAIR):
-                for e in range(PAIR):
-                    nc.sync.dma_start(out=k_sb[e::PAIR, :, u, :], in_=k_rows[u, e])
+            k_sb = raw.tile([P, PLANES, D], BF16, tag="k_sb")
+            nc.sync.dma_start(out=k_sb[:], in_=K[0, h].rearrange("(c p) d -> p c d", p=P))
             q_sb = raw.tile([P, NJ, D], BF16, tag="q_sb")
             nc.sync.dma_start(out=q_sb[:], in_=Q[0, h].rearrange("(p j) d -> p j d", j=NJ))
             live["k_sb", h] = k_sb
@@ -83,19 +81,16 @@ def tile_scaleddotproductattention_kernel(tc, Q, K, V, mask, out):
 
         def load_v(h):
             v_sb = raw.tile([P, G, PACK, D], BF16, tag="v_sb")
-            nc.sync.dma_start(out=v_sb[:], in_=V[0, h].rearrange("(g p t) d -> p g t d", g=G, t=PACK))
+            nc.sync.dma_start(
+                out=v_sb[:].rearrange("p g (u e) d -> p (g u) e d", u=PAIR),
+                in_=V[0, h].rearrange("(a p e) d -> p a e d", a=WB, e=PAIR),
+            )
             live["v_sb", h] = v_sb
 
         def transpose_k(h):
             pk = psum.tile([P, PLANES, P], BF16, tag="bank")
-            for g in range(G):
-                for u in range(PAIR):
-                    for b in range(PAIR):
-                        nc.tensor.transpose(
-                            out=pk[:, (g * PAIR + u) * PAIR + b, :],
-                            in_=live["k_sb", h][:, g * PAIR + b, u, :],
-                            identity=ident_bf[:],
-                        )
+            for i in range(PLANES):
+                nc.tensor.transpose(out=pk[:, i, :], in_=live["k_sb", h][:, i, :], identity=ident_bf[:])
             live["pk", h] = pk
 
         def transpose_q(h):
@@ -104,16 +99,10 @@ def tile_scaleddotproductattention_kernel(tc, Q, K, V, mask, out):
                 nc.tensor.transpose(out=pq[:, j, :], in_=live["q_sb", h][:, j, :], identity=ident_bf[:])
             live["pq", h] = pq
 
-        def on_scalar(h):
-            return h % 2 == 1
-
         def copy_k(h):
             k_t = heads.tile([P, N], BF16, tag="k_t")
             k_ps = live["pk", h][:].rearrange("d c p -> d (c p)")
-            if on_scalar(h):
-                nc.scalar.copy(out=k_t[:], in_=k_ps)
-            else:
-                nc.vector.tensor_copy(out=k_t[:], in_=k_ps)
+            nc.scalar.copy(out=k_t[:], in_=k_ps)
             live["k_t", h] = k_t
 
         def copy_q(h):
@@ -148,48 +137,61 @@ def tile_scaleddotproductattention_kernel(tc, Q, K, V, mask, out):
 
 
         def load_mask(j):
-            mi = mstage.tile([P, 2 * N], I32, tag="mi", bufs=NJ)
+            mi = mstage.tile([P, 8 * N], U8, tag="mi", bufs=NJ)
+            half = 8 * N // G
             for g in range(G):
-                nc.sync.dma_start(out=mi[:, g * N : (g + 1) * N], in_=mask_words[:, j, g * N : (g + 1) * N])
+                cols = slice(g * half, (g + 1) * half)
+                if j < EARLY:
+                    nc.sync.dma_start(
+                        out=mi[:, cols].bitcast(I32), in_=mask_words[:, j, g * N : (g + 1) * N]
+                    )
+                else:
+                    nc.sync.dma_start(out=mi[:, cols], in_=mask_bytes[j - 1 : N - 1 : NJ, cols])
             live["mi", j] = mi
 
         def convert_mask(j):
-            mf = mstage.tile([P, G, PACK, P], BF16, tag="mf", bufs=NJ)
-            words = live["mi", j][:].rearrange(
-                "q (g b r u e w) -> q g u b r e w", g=G, b=PAIR, r=P // PAIR, u=PAIR, e=PAIR, w=2
-            )
+            mf = mstage.tile([P, N], BF16, tag="mf", bufs=EARLY)
+            words = live["mi", j][:].bitcast(I32).rearrange("q (k w) -> q k w", w=2)
             for g in range(G):
-                for u in range(PAIR):
-                    nc.vector.tensor_scalar(
-                        out=mf[:, g, u * PAIR : (u + 1) * PAIR, :].rearrange("q b (r e) -> q b r e", e=PAIR),
-                        in0=words[:, g, u, :, :, :, 0],
-                        scalar1=MASKED,
-                        scalar2=None,
-                        op0=ALU.mult,
-                    )
+                keys = slice(g * BANK, (g + 1) * BANK)
+                nc.vector.tensor_scalar(
+                    out=mf[:, keys], in0=words[:, keys, 0], scalar1=MASKED, scalar2=None, op0=ALU.mult
+                )
             live["mf", j] = mf
 
         def transpose_mask(j):
             pm = psum.tile([P, PLANES, P], BF16, tag="bank")
-            for c in range(PLANES):
-                nc.tensor.transpose(
-                    out=pm[:, c, :], in_=live["mf", j][:, c // PACK, c % PACK, :], identity=ident_bf[:]
-                )
+            if j < EARLY:
+                keys_of = live["mf", j][:]
+            else:
+                keys_of = live["mi", j][:].bitcast(BF16).rearrange("q (k w) -> q k w", w=4)[:, :, 0]
+            for i in range(PLANES):
+                nc.tensor.transpose(out=pm[:, i, :], in_=keys_of[:, i * P : (i + 1) * P], identity=ident_bf[:])
             live["pm", j] = pm
 
         def copy_mask(j):
-            nc.scalar.copy(out=mask_t[:, :, j, :], in_=live["pm", j][:])
+            if j < EARLY:
+                nc.scalar.copy(out=mask_t[:, :, j, :], in_=live["pm", j][:])
+            else:
+                nc.vector.tensor_scalar(
+                    out=mask_t[:, :, j, :],
+                    in0=live["pm", j][:],
+                    scalar1=2.0**125,
+                    scalar2=MASKED,
+                    op0=ALU.mult,
+                    op1=ALU.mult,
+                )
 
 
         def mask_scores(i, g):
             h, j = head_and_tile(i)
             sp = psum.tile([P, BANK], F32, tag="bank")
             live["sp", i, g] = sp
-            if i < MATMUL_MASKED:
+            if i < 2 * EARLY:
                 nc.tensor.matmul(
                     out=sp[:],
                     lhsT=ident_bf[:],
-                    rhs=live["mf", j][:, g].rearrange("q t p -> q (t p)"),
+                    rhs=live["mf", j][:, g * BANK : (g + 1) * BANK],
                     start=True,
                     stop=False,
                 )
@@ -268,7 +270,8 @@ def tile_scaleddotproductattention_kernel(tc, Q, K, V, mask, out):
                 live["grouped", b] = batch.tile(
                     [P, UB, G, P, PACK], BF16, tag="grouped", align_bytes=64, bufs=3, name="grouped"
                 )
-            nc.scalar.copy(
+            copy = nc.vector.tensor_copy if UNITS - 3 <= i < UNITS - 1 else nc.scalar.copy
+            copy(
                 out=live["grouped", b][:, u]
                 .rearrange("p g q t -> p (g q t)")
                 .bitcast(F32)
@@ -277,16 +280,16 @@ def tile_scaleddotproductattention_kernel(tc, Q, K, V, mask, out):
             )
 
 
-        def quantise_e(b):
-            codes = batch.tile([P, UB, G, P], U32, tag="codes", align_bytes=64, bufs=2)
-            scales = batch.tile([P, UB, G, P], U8, tag="scales", align_bytes=64, bufs=2)
+        def quantise_e(b, u0, count):
+            if u0 == 0:
+                live["codes", b] = batch.tile([P, UB, G, P], U32, tag="codes", align_bytes=64, bufs=2, name="codes")
+                live["scales", b] = batch.tile([P, UB, G, P], U8, tag="scales", align_bytes=64, bufs=2, name="scales")
+            units = slice(u0, u0 + count)
             nc.vector.quantize_mx(
-                out=codes[:].rearrange("p i g q -> p (i g q)").bitcast(FP8X4),
-                scales=scales[:].rearrange("p i g q -> p (i g q)"),
-                in_=live["grouped", b][:].rearrange("p i g q t -> p (i g q t)"),
+                out=live["codes", b][:, units].rearrange("p i g q -> p (i g q)").bitcast(FP8X4),
+                scales=live["scales", b][:, units].rearrange("p i g q -> p (i g q)"),
+                in_=live["grouped", b][:, units].rearrange("p i g q t -> p (i g q t)"),
             )
-            live["codes", b] = codes
-            live["scales", b] = scales
 
         def reciprocals(b):
             if b % 2 == 1:
@@ -294,13 +297,13 @@ def tile_scaleddotproductattention_kernel(tc, Q, K, V, mask, out):
                 nc.vector.reciprocal(out=rinv[:], in_=live["rowsum", b // 2][:])
                 live["rinv", b // 2] = rinv
 
-        def e_times_v(b):
-            o_ps = psum.tile([P, UB, D], F32, tag="bank")
-            for u in range(UB):
+        def e_times_v(b, u0, count):
+            o_ps = psum.tile([P, count, D], F32, tag="bank")
+            for u in range(u0, u0 + count):
                 h, j = head_and_tile(b * UB + u)
                 for g in range(G):
                     nc.tensor.matmul_mx(
-                        out=o_ps[:, u, :],
+                        out=o_ps[:, u - u0, :],
                         lhsT=live["codes", b][:, u, g, :].bitcast(FP8X4),
                         lhsT_scale=live["scales", b][:, u, g, :],
                         rhs=live["v_codes", h][:, g * D : (g + 1) * D].bitcast(FP8X4),
@@ -308,24 +311,25 @@ def tile_scaleddotproductattention_kernel(tc, Q, K, V, mask, out):
                         start=(g == 0),
                         stop=(g == G - 1),
                     )
-            live["o_ps", b] = o_ps
+            live["o_ps", b, u0] = o_ps
 
-        def divide_and_store(b):
+        def divide_and_store(b, u0, count):
             o_sb = batch.tile([P, UB, D], F32, tag="o_sb")
+            rinv = live["rinv", b // 2][:, b % 2, u0 : u0 + count]
             nc.vector.tensor_tensor(
-                out=o_sb[:],
-                in0=live["o_ps", b][:],
-                in1=live["rinv", b // 2][:, b % 2, :].unsqueeze(2).to_broadcast([P, UB, D]),
+                out=o_sb[:, :count],
+                in0=live["o_ps", b, u0][:],
+                in1=rinv.unsqueeze(2).to_broadcast([P, count, D]),
                 op=ALU.mult,
             )
-            h, j0 = head_and_tile(b * UB)
+            h, j0 = head_and_tile(b * UB + u0)
             if b * UB < PAIRED:
                 for h in range(2):
                     rows = out[0, h].rearrange("(p j) d -> p j d", j=NJ)
                     nc.sync.dma_start(out=rows[:, j0 : j0 + 2, :], in_=o_sb[:, h::2, :])
             else:
                 rows = out[0, h].rearrange("(p j) d -> p j d", j=NJ)
-                nc.sync.dma_start(out=rows[:, j0 : j0 + UB, :], in_=o_sb[:])
+                nc.sync.dma_start(out=rows[:, j0 : j0 + count, :], in_=o_sb[:, :count])
 
 
         def unit_at(k, lag):
@@ -334,6 +338,14 @@ def tile_scaleddotproductattention_kernel(tc, Q, K, V, mask, out):
         def batch_at(k, lag):
             b, u = divmod(k - lag, UB)
             return b if u == UB - 1 and 0 <= b < BATCHES else None
+
+        def run_batch(stage, k, lag):
+            b, u = divmod(k - lag, UB)
+            if u == UB - 1 and 0 <= b < BATCHES - 1:
+                stage(b, 0, UB)
+            b, u = divmod(k - lag + 1, UB)
+            if b == BATCHES - 1:
+                stage(b, u, 1)
 
         def first_unit(h):
             return h if h < 2 else h * NJ
@@ -352,10 +364,10 @@ def tile_scaleddotproductattention_kernel(tc, Q, K, V, mask, out):
             return next_of(H, lambda h: first_unit(h) - (1 if h < 2 else 2) == k)
 
         def mask_tile_to_convert(k):
-            return next_of(NJ, lambda j: max(0, min(2 * j - 1, j + 3)) == k)
+            return next_of(EARLY, lambda j: max(0, 2 * j - 1) == k)
 
         def mask_tile_at(k, lag):
-            return k - lag if 0 <= k - lag < NJ else None
+            return next_of(NJ, lambda j: (2 * j + 7 if j < EARLY else 2 * j - 2) + lag == k)
 
         def run(stage, index, *more):
             if index is not None:
@@ -366,9 +378,11 @@ def tile_scaleddotproductattention_kernel(tc, Q, K, V, mask, out):
         load_mask(0)
         load_k_and_q(1)
         load_mask(1)
+        load_mask(2)
+        load_mask(3)
         load_v(0)
         load_v(1)
-        for j in range(2, NJ):
+        for j in range(4, NJ):
             load_mask(j)
 
         for k in range(-1, LAST_STEP + 1):
@@ -377,32 +391,28 @@ def tile_scaleddotproductattention_kernel(tc, Q, K, V, mask, out):
                 load_k_and_q(h)
                 load_v(h)
             run(row_max, unit_at(k, LAG_MAX), 0)
-            run(quantise_e, batch_at(k, LAG_QUANTISE))
-            run(quantise_v, head_at(k, 6))
+            run_batch(quantise_e, k, LAG_QUANTISE)
+            run(quantise_v, head_at(k, 7))
             run(row_max, unit_at(k, LAG_MAX), 1)
             run(join_row_max, unit_at(k, LAG_MAX))
-            k_head = head_with_k(k - 1)
-            if k_head is not None and not on_scalar(k_head):
-                copy_k(k_head)
             run(convert_mask, mask_tile_to_convert(k))
             for h in range(H):
-                piece = k - first_unit(h) - 2
+                piece = k - first_unit(h) - 3
                 if 0 <= piece < PACK:
                     group_v(h, piece)
             run(exponent, unit_at(k, LAG_EXP))
-            if k_head is not None and on_scalar(k_head):
-                copy_k(k_head)
+            run(copy_k, head_with_k(k - 1))
             run(copy_q, head_with_q(k - 1))
             run(copy_e, unit_at(k, LAG_COPY))
-            run(copy_mask, mask_tile_at(k, 4))
-            run(divide_and_store, batch_at(k, LAG_DIVIDE))
+            run(copy_mask, mask_tile_at(k, 1))
+            run_batch(divide_and_store, k, LAG_DIVIDE)
             run(reciprocals, batch_at(k, LAG_RECIPROCAL))
             run(mask_scores, unit_at(k, 0), 0)
             run(mask_scores, unit_at(k, 0), 1)
             run(q_times_k, unit_at(k, 0), 0)
-            run(e_times_v, batch_at(k, LAG_PV))
+            run_batch(e_times_v, k, LAG_PV)
             run(q_times_k, unit_at(k, 0), 1)
             run(transpose_e, unit_at(k, LAG_TRANSPOSE), range(WB))
-            run(transpose_mask, mask_tile_at(k, 3))
+            run(transpose_mask, mask_tile_at(k, 0))
             run(transpose_k, head_with_k(k))
             run(transpose_q, head_with_q(k))

@@ -34,13 +34,13 @@ EARLY = 3
 FLOPS = 4 * H * N * N * D
 
 LAG_MAX = 1
-LAG_EXP = 3
-LAG_TRANSPOSE = 4
-LAG_COPY = 5
-LAG_QUANTISE = 7
-LAG_RECIPROCAL = 4
-LAG_PV = 8
-LAG_DIVIDE = 9
+LAG_EXP = 4
+LAG_TRANSPOSE = 5
+LAG_COPY = 6
+LAG_QUANTISE = 8
+LAG_RECIPROCAL = 5
+LAG_PV = 9
+LAG_DIVIDE = 10
 LAST_STEP = UNITS - 1 + LAG_DIVIDE
 
 
@@ -51,8 +51,8 @@ def tile_scaleddotproductattention_kernel(tc, Q, K, V, mask, out):
         mstage = ctx.enter_context(tc.tile_pool(name="mstage", bufs=2))
         raw = ctx.enter_context(tc.tile_pool(name="raw", bufs=3))
         heads = ctx.enter_context(tc.tile_pool(name="heads", bufs=3))
-        work = ctx.enter_context(tc.tile_pool(name="work", bufs=4))
-        small = ctx.enter_context(tc.tile_pool(name="small", bufs=5))
+        work = ctx.enter_context(tc.tile_pool(name="work", bufs=6))
+        small = ctx.enter_context(tc.tile_pool(name="small", bufs=8))
         batch = ctx.enter_context(tc.tile_pool(name="batch", bufs=3))
         psum = ctx.enter_context(tc.psum_pool(name="psum", bufs=8))
         ctx.enter_context(tc.manual_schedule())
@@ -392,7 +392,7 @@ def tile_scaleddotproductattention_kernel(tc, Q, K, V, mask, out):
                 load_v(h)
             run(row_max, unit_at(k, LAG_MAX), 0)
             run_batch(quantise_e, k, LAG_QUANTISE)
-            run(quantise_v, head_at(k, 7))
+            run(quantise_v, head_at(k, 10))
             run(row_max, unit_at(k, LAG_MAX), 1)
             run(join_row_max, unit_at(k, LAG_MAX))
             run(convert_mask, mask_tile_to_convert(k))

import math
from contextlib import ExitStack

import concourse.mybir as mybir
from concourse.masks import make_identity

FP8X4 = mybir.dt.float8_e4m3fn_x4
BF16 = mybir.dt.bfloat16
F32 = mybir.dt.float32
I32 = mybir.dt.int32
U32 = mybir.dt.uint32
U8 = mybir.dt.uint8
ALU = mybir.AluOpType
ACTF = mybir.ActivationFunctionType

P = 128
H = 16
N = 1024
D = 128
NJ = N // P
PACK = 4
G = N // (P * PACK)
PLANES = G * PACK
PAIR = 2
WB = PLANES // PAIR
BANK = PACK * P
UB = 4
UNITS = H * NJ
BATCHES = UNITS // UB
SCALE = 1.0 / math.sqrt(D)
MASKED = -(2.0**43)
PAIRED = 2 * NJ
EARLY = 3
FLOPS = 4 * H * N * N * D

LAG_MAX = 1
LAG_EXP = 4
LAG_TRANSPOSE = 5
LAG_COPY = 6
LAG_QUANTISE = 8
LAG_RECIPROCAL = 5
LAG_PV = 9
LAG_DIVIDE = 10
LAST_STEP = UNITS - 1 + LAG_DIVIDE


def tile_scaleddotproductattention_kernel(tc, Q, K, V, mask, out):
    nc = tc.nc
    with ExitStack() as ctx:
        const = ctx.enter_context(tc.tile_pool(name="const", bufs=1))
        mstage = ctx.enter_context(tc.tile_pool(name="mstage", bufs=2))
        raw = ctx.enter_context(tc.tile_pool(name="raw", bufs=3))
        heads = ctx.enter_context(tc.tile_pool(name="heads", bufs=3))
        work = ctx.enter_context(tc.tile_pool(name="work", bufs=6))
        small = ctx.enter_context(tc.tile_pool(name="small", bufs=8))
        batch = ctx.enter_context(tc.tile_pool(name="batch", bufs=3))
        psum = ctx.enter_context(tc.psum_pool(name="psum", bufs=8))
        ctx.enter_context(tc.manual_schedule())

        ident_bf = const.tile([P, P], BF16)
        make_identity(nc, ident_bf[:])
        ident_f = const.tile([P, P], F32)
        make_identity(nc, ident_f[:])
        mask_t = const.tile([P, PLANES, NJ, P], F32)
        mask_words = mask.bitcast(I32).rearrange("(p j) w -> p j w", j=NJ)
        mask_bytes = mask.bitcast(U8).rearrange("q b -> (q b)")[8 * N - 1 : 8 * N * N - 1].rearrange("(r b) -> r b", b=8 * N)

        def head_and_tile(i):
            return (i % 2, i // 2) if i < PAIRED else divmod(i, NJ)

        live = {}


        def load_k_and_q(h):
            k_sb = raw.tile([P, PLANES, D], BF16, tag="k_sb")
            nc.sync.dma_start(out=k_sb[:], in_=K[0, h].rearrange("(c p) d -> p c d", p=P))
            q_sb = raw.tile([P, NJ, D], BF16, tag="q_sb")
            nc.sync.dma_start(out=q_sb[:], in_=Q[0, h].rearrange("(p j) d -> p j d", j=NJ))
            live["k_sb", h] = k_sb
            live["q_sb", h] = q_sb

        def load_v(h):
            v_sb = raw.tile([P, G, PACK, D], BF16, tag="v_sb")
            nc.sync.dma_start(
                out=v_sb[:].rearrange("p g (u e) d -> p (g u) e d", u=PAIR),
                in_=V[0, h].rearrange("(a p e) d -> p a e d", a=WB, e=PAIR),
            )
            live["v_sb", h] = v_sb

        def transpose_k(h):
            pk = psum.tile([P, PLANES, P], BF16, tag="bank")
            for i in range(PLANES):
                nc.tensor.transpose(out=pk[:, i, :], in_=live["k_sb", h][:, i, :], identity=ident_bf[:])
            live["pk", h] = pk

        def transpose_q(h):
            pq = psum.tile([P, NJ, P], BF16, tag="bank")
            for j in range(NJ):
                nc.tensor.transpose(out=pq[:, j, :], in_=live["q_sb", h][:, j, :], identity=ident_bf[:])
            live["pq", h] = pq

        def copy_k(h):
            k_t = heads.tile([P, N], BF16, tag="k_t")
            k_ps = live["pk", h][:].rearrange("d c p -> d (c p)")
            nc.scalar.copy(out=k_t[:], in_=k_ps)
            live["k_t", h] = k_t

        def copy_q(h):
            q_t = heads.tile([P, NJ, P], BF16, tag="q_t")
            nc.scalar.copy(out=q_t[:], in_=live["pq", h][:])
            live["q_t", h] = q_t

        def group_v(h, piece):
            if piece == 0:
                live["v_g", h] = heads.tile([P, G, D, PACK], BF16, tag="v_g", align_bytes=64, name="v_g")
            g, half = divmod(piece, 2)
            cols = slice(half * D // 2, (half + 1) * D // 2)
            nc.gpsimd.tensor_scalar(
                out=live["v_g", h][:, g, cols, :],
                in0=live["v_sb", h][:, g, :, cols].rearrange("p t d -> p d t"),
                scalar1=1.0,
                scalar2=0.0,
                op0=ALU.mult,
                op1=ALU.add,
            )

        def quantise_v(h):
            v_codes = heads.tile([P, G * D], U32, tag="v_codes", align_bytes=64)
            v_scales = heads.tile([P, G * D], U8, tag="v_scales", align_bytes=64)
            nc.vector.quantize_mx(
                out=v_codes[:].bitcast(FP8X4),
                scales=v_scales[:],
                in_=live["v_g", h][:].rearrange("p g d t -> p (g d t)"),
            )
            live["v_codes", h] = v_codes
            live["v_scales", h] = v_scales


        def load_mask(j):
            mi = mstage.tile([P, 8 * N], U8, tag="mi", bufs=NJ)
            half = 8 * N // G
            for g in range(G):
                cols = slice(g * half, (g + 1) * half)
                if j < EARLY:
                    nc.sync.dma_start(
                        out=mi[:, cols].bitcast(I32), in_=mask_words[:, j, g * N : (g + 1) * N]
                    )
                else:
                    nc.sync.dma_start(out=mi[:, cols], in_=mask_bytes[j - 1 : N - 1 : NJ, cols])
            live["mi", j] = mi

        def convert_mask(j):
            mf = mstage.tile([P, N], BF16, tag="mf", bufs=EARLY)
            words = live["mi", j][:].bitcast(I32).rearrange("q (k w) -> q k w", w=2)
            for g in range(G):
                keys = slice(g * BANK, (g + 1) * BANK)
                nc.vector.tensor_scalar(
                    out=mf[:, keys], in0=words[:, keys, 0], scalar1=MASKED, scalar2=None, op0=ALU.mult
                )
            live["mf", j] = mf

        def transpose_mask(j):
            pm = psum.tile([P, PLANES, P], BF16, tag="bank")
            if j < EARLY:
                keys_of = live["mf", j][:]
            else:
                keys_of = live["mi", j][:].bitcast(BF16).rearrange("q (k w) -> q k w", w=4)[:, :, 0]
            for i in range(PLANES):
                nc.tensor.transpose(out=pm[:, i, :], in_=keys_of[:, i * P : (i + 1) * P], identity=ident_bf[:])
            live["pm", j] = pm

        def copy_mask(j):
            if j < EARLY:
                nc.scalar.copy(out=mask_t[:, :, j, :], in_=live["pm", j][:])
            else:
                nc.vector.tensor_scalar(
                    out=mask_t[:, :, j, :],
                    in0=live["pm", j][:],
                    scalar1=2.0**125,
                    scalar2=MASKED,
                    op0=ALU.mult,
                    op1=ALU.mult,
                )


        def mask_scores(i, g):
            h, j = head_and_tile(i)
            sp = psum.tile([P, BANK], F32, tag="bank")
            live["sp", i, g] = sp
            if i < 2 * EARLY:
                nc.tensor.matmul(
                    out=sp[:],
                    lhsT=ident_bf[:],
                    rhs=live["mf", j][:, g * BANK : (g + 1) * BANK],
                    start=True,
                    stop=False,
                )
                return
            for t in range(PACK):
                nc.tensor.matmul(
                    out=sp[:, t * P : (t + 1) * P],
                    lhsT=mask_t[:, g * PACK + t, j, :],
                    rhs=ident_f[:],
                    is_transpose=True,
                    start=(t == 0),
                    stop=False,
                )

        def q_times_k(i, g):
            h, j = head_and_tile(i)
            nc.tensor.matmul(
                out=live["sp", i, g][:],
                lhsT=live["q_t", h][:, j, :],
                rhs=live["k_t", h][:, g * BANK : (g + 1) * BANK],
                start=False,
                stop=True,
            )

        def row_max(i, g):
            if g == 0:
                live["neg_s", i] = work.tile([P, G, BANK], F32, tag="neg_s", name="neg_s")
                live["neg_m2", i] = small.tile([P, G], F32, tag="neg_m2", name="neg_m2")
            nc.vector.tensor_scalar(
                out=live["neg_s", i][:, g, :],
                in0=live["sp", i, g][:],
                scalar1=-SCALE,
                scalar2=None,
                op0=ALU.mult,
                op1=ALU.min,
                accum_out=live["neg_m2", i][:, g : g + 1],
            )

        def join_row_max(i):
            neg_m = small.tile([P, 1], F32, tag="neg_m")
            nc.gpsimd.tensor_scalar(
                out=neg_m[:],
                in0=live["neg_m2", i][:, 0:1],
                scalar1=live["neg_m2", i][:, 1:2],
                scalar2=-3.0e38,
                op0=ALU.min,
                op1=ALU.max,
            )
            live["neg_m", i] = neg_m

        def exponent(i):
            b, u = divmod(i, UB)
            if i % (2 * UB) == 0:
                live["rowsum", b // 2] = batch.tile([P, 2, UB], F32, tag="rowsum", name="rowsum")
            e = work.tile([P, N], BF16, tag="e")
            nc.scalar.activation(
                out=e[:],
                in_=live["neg_s", i][:].rearrange("q g c -> q (g c)"),
                func=ACTF.Exp,
                bias=live["neg_m", i][:, 0:1],
                scale=-1.0,
                accum_out=live["rowsum", b // 2][:, b % 2, u : u + 1],
            )
            live["e", i] = e

        def transpose_e(i, blocks):
            if ("et", i) not in live:
                live["et", i] = psum.tile([P, WB, P], F32, tag="bank", name="et")
            e_words = live["e", i][:].bitcast(F32)
            for a in blocks:
                nc.tensor.transpose(out=live["et", i][:, a, :], in_=e_words[:, a * P : (a + 1) * P], identity=ident_f[:])

        def copy_e(i):
            b, u = divmod(i, UB)
            if u == 0:
                live["grouped", b] = batch.tile(
                    [P, UB, G, P, PACK], BF16, tag="grouped", align_bytes=64, bufs=3, name="grouped"
                )
            copy = nc.vector.tensor_copy if UNITS - 3 <= i < UNITS - 1 else nc.scalar.copy
            copy(
                out=live["grouped", b][:, u]
                .rearrange("p g q t -> p (g q t)")
                .bitcast(F32)
                .rearrange("p (g q u) -> p g q u", g=G, u=PAIR),
                in_=live["et", i][:].rearrange("p (g u) q -> p g q u", u=PAIR),
            )


        def quantise_e(b, u0, count):
            if u0 == 0:
                live["codes", b] = batch.tile([P, UB, G, P], U32, tag="codes", align_bytes=64, bufs=2, name="codes")
                live["scales", b] = batch.tile([P, UB, G, P], U8, tag="scales", align_bytes=64, bufs=2, name="scales")
            units = slice(u0, u0 + count)
            nc.vector.quantize_mx(
                out=live["codes", b][:, units].rearrange("p i g q -> p (i g q)").bitcast(FP8X4),
                scales=live["scales", b][:, units].rearrange("p i g q -> p (i g q)"),
                in_=live["grouped", b][:, units].rearrange("p i g q t -> p (i g q t)"),
            )

        def reciprocals(b):
            if b % 2 == 1:
                rinv = batch.tile([P, 2, UB], F32, tag="rinv")
                nc.vector.reciprocal(out=rinv[:], in_=live["rowsum", b // 2][:])
                live["rinv", b // 2] = rinv

        def e_times_v(b, u0, count):
            o_ps = psum.tile([P, count, D], F32, tag="bank")
            for u in range(u0, u0 + count):
                h, j = head_and_tile(b * UB + u)
                for g in range(G):
                    nc.tensor.matmul_mx(
                        out=o_ps[:, u - u0, :],
                        lhsT=live["codes", b][:, u, g, :].bitcast(FP8X4),
                        lhsT_scale=live["scales", b][:, u, g, :],
                        rhs=live["v_codes", h][:, g * D : (g + 1) * D].bitcast(FP8X4),
                        rhs_scale=live["v_scales", h][:, g * D : (g + 1) * D],
                        start=(g == 0),
                        stop=(g == G - 1),
                    )
            live["o_ps", b, u0] = o_ps

        def divide_and_store(b, u0, count):
            o_sb = batch.tile([P, UB, D], F32, tag="o_sb")
            rinv = live["rinv", b // 2][:, b % 2, u0 : u0 + count]
            nc.vector.tensor_tensor(
                out=o_sb[:, :count],
                in0=live["o_ps", b, u0][:],
                in1=rinv.unsqueeze(2).to_broadcast([P, count, D]),
                op=ALU.mult,
            )
            h, j0 = head_and_tile(b * UB + u0)
            if b * UB < PAIRED:
                for h in range(2):
                    rows = out[0, h].rearrange("(p j) d -> p j d", j=NJ)
                    nc.sync.dma_start(out=rows[:, j0 : j0 + 2, :], in_=o_sb[:, h::2, :])
            else:
                rows = out[0, h].rearrange("(p j) d -> p j d", j=NJ)
                nc.sync.dma_start(out=rows[:, j0 : j0 + count, :], in_=o_sb[:, :count])


        def unit_at(k, lag):
            return k - lag if 0 <= k - lag < UNITS else None

        def batch_at(k, lag):
            b, u = divmod(k - lag, UB)
            return b if u == UB - 1 and 0 <= b < BATCHES else None

        def run_batch(stage, k, lag):
            b, u = divmod(k - lag, UB)
            if u == UB - 1 and 0 <= b < BATCHES - 1:
                stage(b, 0, UB)
            b, u = divmod(k - lag + 1, UB)
            if b == BATCHES - 1:
                stage(b, u, 1)

        def first_unit(h):
            return h if h < 2 else h * NJ

        def head_at(k, lag):
            return next_of(H, lambda h: first_unit(h) + lag == k)

        def next_of(count, test):
            found = [n for n in range(count) if test(n)]
            return found[0] if found else None

        def head_with_k(k):
            return next_of(H, lambda h: first_unit(h) - (1 if h < 2 else 3) == k)

        def head_with_q(k):
            return next_of(H, lambda h: first_unit(h) - (1 if h < 2 else 2) == k)

        def mask_tile_to_convert(k):
            return next_of(EARLY, lambda j: max(0, 2 * j - 1) == k)

        def mask_tile_at(k, lag):
            return next_of(NJ, lambda j: (2 * j + 7 if j < EARLY else 2 * j - 2) + lag == k)

        def run(stage, index, *more):
            if index is not None:
                stage(index, *more)


        load_k_and_q(0)
        load_mask(0)
        load_k_and_q(1)
        load_mask(1)
        load_mask(2)
        load_mask(3)
        load_v(0)
        load_v(1)
        for j in range(4, NJ):
            load_mask(j)

        for k in range(-1, LAST_STEP + 1):
            h = head_at(k, -13)
            if h is not None and h > 1:
                load_k_and_q(h)
                load_v(h)
            run(row_max, unit_at(k, LAG_MAX), 0)
            run_batch(quantise_e, k, LAG_QUANTISE)
            run(quantise_v, head_at(k, 10))
            run(row_max, unit_at(k, LAG_MAX), 1)
            run(join_row_max, unit_at(k, LAG_MAX))
            run(convert_mask, mask_tile_to_convert(k))
            for h in range(H):
                piece = k - first_unit(h) - 3
                if 0 <= piece < PACK:
                    group_v(h, piece)
            run(exponent, unit_at(k, LAG_EXP))
            run(copy_k, head_with_k(k - 1))
            run(copy_q, head_with_q(k - 1))
            run(copy_e, unit_at(k, LAG_COPY))
            run(copy_mask, mask_tile_at(k, 1))
            run_batch(divide_and_store, k, LAG_DIVIDE)
            run(reciprocals, batch_at(k, LAG_RECIPROCAL))
            run(mask_scores, unit_at(k, 0), 0)
            run(mask_scores, unit_at(k, 0), 1)
            run(q_times_k, unit_at(k, 0), 0)
            run_batch(e_times_v, k, LAG_PV)
            run(q_times_k, unit_at(k, 0), 1)
            run(transpose_e, unit_at(k, LAG_TRANSPOSE), range(WB))
            run(transpose_mask, mask_tile_at(k, 0))
            run(transpose_k, head_with_k(k))
            run(transpose_q, head_with_q(k))
